import numpy as np
import ml_dtypes


def mxq(x, axis, fmt="e4m3"):
    dtype, down = {"e4m3": (ml_dtypes.float8_e4m3fn, 7), "e5m2": (ml_dtypes.float8_e5m2, 14)}[fmt]
    v = np.moveaxis(np.asarray(x, np.float32).astype(ml_dtypes.bfloat16).astype(np.float64), axis, -1)
    blocks = v.reshape(v.shape[:-1] + (-1, 32))
    amax = np.abs(blocks).max(-1, keepdims=True)
    byte = np.maximum(np.where(amax > 0, np.frexp(amax)[1] - 1 + 127, 0) - down, 1)
    scale = np.exp2(byte - 127.0)
    codes = (blocks / scale).astype(np.float32).astype(dtype).astype(np.float64)
    return np.moveaxis((codes * scale).reshape(v.shape), -1, axis)


WIDE = False


def mx_kscale(k):
    if not WIDE:
        return np.ones(k)
    levels = np.array([10, -10, 5, -5, 0])
    a = np.random.permutation(np.resize(levels, k // 512 * 4)).reshape(k // 512, 4)
    idx = np.arange(k)
    return np.exp2(a[idx // 512, idx % 128 // 32])


BF16 = ml_dtypes.bfloat16


def bf(x):
    return np.asarray(x, np.float32).astype(BF16)


def f64(x):
    return np.asarray(x).astype(np.float64)


B, N, L, M, F = 2, 8, 16384, 128, 64
EPS = 1e-8
KAPPA0 = -3.0


def softplus(v):
    return np.logaddexp(v, 0.0)


def sigmoid(v):
    return 1.0 / (1.0 + np.exp(-v))


def setup_inputs():
    e = np.log2(mx_kscale(L))
    keep = np.abs(e) == np.abs(e).min()
    k0 = softplus(KAPPA0)
    t = np.zeros(L)
    t[keep] = np.sort(np.random.uniform(0.0, 1.0, int(keep.sum())))
    off = k0 * (np.log(2.0) * 2.0 * np.abs(e) + np.random.uniform(0.0, 1.0, L))
    t = np.where(keep, t, np.where(e > 0, 1.0 + off, -off))[:, None]
    t_left = np.random.uniform(0.0, 1.0, (N, M)) * 0.8
    t_right = t_left + 0.05 + 0.15 * np.random.uniform(0.0, 1.0, (N, M))
    kappa = KAPPA0 + 0.3 * np.random.standard_normal((N, 1))
    tq = f64(bf(t))[:, 0]
    kq = softplus(f64(bf(kappa)))
    d = np.maximum(np.maximum(tq - 1.0, -tq), 0.0)
    g = np.where(d > 0.0, 0.5, 1.0) * np.exp(d[None, :] / kq)
    x_aug = np.random.standard_normal((B, N, L, F)) * 0.15 * np.sqrt(L) * g[None, :, :, None]
    return {"x_aug": bf(x_aug), "t": bf(t), "t_left": bf(t_left), "t_right": bf(t_right), "kappa": bf(kappa)}


def reference(x_aug, t, t_left, t_right, kappa):
    t = f64(t)
    k = softplus(f64(kappa))[None, :, None]
    tl = f64(t_left)[None, :, None, :]
    tr = f64(t_right)[None, :, None, :]
    alpha = sigmoid((tr - t) / k) * sigmoid((t - tl) / k)
    numerator = mxq(alpha[0], 1, "e4m3").transpose(0, 2, 1) @ mxq(f64(x_aug), 2, "e4m3")
    denominator = alpha.sum(axis=2)[..., None]
    return numerator / (denominator + EPS)

@@ -1,0 +1,416 @@
+from contextlib import ExitStack
+
+import concourse.mybir as mybir
+from concourse.masks import make_identity
+
+F32 = mybir.dt.float32
+BF16 = mybir.dt.bfloat16
+I32 = mybir.dt.int32
+U32 = mybir.dt.uint32
+U8 = mybir.dt.uint8
+FP8X4 = mybir.dt.float8_e4m3fn_x4
+FUNC = mybir.ActivationFunctionType
+ALU = mybir.AluOpType
+AXIS_X = mybir.AxisListType.X
+
+B, N, L, M, F = 2, 8, 16384, 128, 64
+EPS = 1e-8
+FLOPS = 2 * B * N * M * F * L
+
+LN2 = 0.6931471805599453
+LN2_HIGH = 0.693145751953125
+LN2_LOW = LN2 - LN2_HIGH
+LOG2_E = 1.4426950408889634
+EXP_TERMS = 12
+ATANH_TERMS = 9
+MOST_NEGATIVE = -80.0
+
+P = 128
+PACK = 4
+PASS_TIMES = P * PACK
+WINDOWS = P // PACK
+GROUPS = M // WINDOWS
+COLS = L // PACK
+STEP_COLS = 2048
+BLOCKS_PER_N = COLS // STEP_COLS
+STEPS = N * BLOCKS_PER_N * GROUPS
+BANK_PASSES = 2
+BANK_COLS = BANK_PASSES * M * PACK
+PAIR_PASSES = 2 * BANK_PASSES
+HALF_PASSES = 2 * PAIR_PASSES
+HALVES = N * L // (PASS_TIMES * HALF_PASSES)
+HALVES_PER_N = HALVES // N
+HALF_WORDS = HALF_PASSES * P
+QUAD = 4
+VECTOR_BANKS = 3
+X_LEAD = 1
+X_LOADS_AHEAD = 4
+SHIFT_COLS = 1024
+
+TRANSPOSE_LAG = GROUPS
+EMPTY_LAG = TRANSPOSE_LAG + 1
+QUANTISE_LAG = EMPTY_LAG + 2
+MULTIPLY_LAG = QUANTISE_LAG + 1
+
+
+def tile_weightedaggregation_k_kernel(tc, x_aug, t, t_left, t_right, kappa, out):
+    nc = tc.nc
+    with ExitStack() as ctx:
+        ctx.enter_context(tc.manual_schedule())
+        const = ctx.enter_context(tc.tile_pool(name="const", bufs=1))
+        shift_pool = ctx.enter_context(tc.tile_pool(name="shift", bufs=2))
+        sig_pool = ctx.enter_context(tc.tile_pool(name="sig", bufs=3))
+        at_pool = ctx.enter_context(tc.tile_pool(name="alpha_t", bufs=2))
+        ag_pool = ctx.enter_context(tc.tile_pool(name="alpha_grouped", bufs=2))
+        aq_pool = ctx.enter_context(tc.tile_pool(name="alpha_q", bufs=3))
+        xr_pool = ctx.enter_context(tc.tile_pool(name="x_raw", bufs=X_LOADS_AHEAD))
+        xg_pool = ctx.enter_context(tc.tile_pool(name="x_grouped", bufs=2))
+        xq_pool = ctx.enter_context(tc.tile_pool(name="x_q", bufs=X_LEAD + 4))
+        bank_pool = ctx.enter_context(tc.psum_pool(name="banks", bufs=4))
+        sum_pool = ctx.enter_context(tc.psum_pool(name="sums", bufs=1))
+
+        t_flat = t.rearrange("l o -> (l o)")
+        shift_run = PACK * (SHIFT_COLS - 1) + 1
+        shifted = {}
+
+        def load_shifted(r):
+            run = shift_pool.tile([P, PACK * SHIFT_COLS], BF16)
+            for j in range(PACK):
+                start = PACK * SHIFT_COLS * r + j
+                nc.sync.dma_start(
+                    out=run[j:P:PACK, 0:shift_run],
+                    in_=t_flat[start : start + shift_run].partition_broadcast(WINDOWS),
+                )
+            shifted[r] = run
+
+        x_raw = {}
+
+        def load_x(half):
+            n, part = divmod(half, HALVES_PER_N)
+            rows = slice(part * HALF_PASSES * PASS_TIMES, (part + 1) * HALF_PASSES * PASS_TIMES)
+            raw = xr_pool.tile([P, B, HALF_PASSES, PACK * F], BF16)
+            for b in range(B):
+                nc.sync.dma_start(
+                    out=raw[:, b],
+                    in_=x_aug[b, n, rows, :].rearrange("(c p j) f -> p c (j f)", p=P, j=PACK),
+                )
+            x_raw[half] = raw
+
+        kappa_b = const.tile([P, N], BF16)
+        nc.scalar.dma_start(out=kappa_b[:], in_=kappa.rearrange("n o -> (n o)").partition_broadcast(P))
+        edge_rows = N * GROUPS
+        edges_b = const.tile([2 * edge_rows, WINDOWS], BF16)
+        nc.scalar.dma_start(
+            out=edges_b[0:edge_rows, :], in_=t_right.rearrange("n (g w) -> (n g) w", w=WINDOWS)
+        )
+        nc.scalar.dma_start(
+            out=edges_b[edge_rows : 2 * edge_rows, :],
+            in_=t_left.rearrange("n (g w) -> (n g) w", w=WINDOWS),
+        )
+        load_shifted(0)
+        load_shifted(1)
+        load_x(0)
+        load_x(1)
+
+        warm = const.tile([P, 1], F32)
+        nc.vector.memset(warm[:], 0.0)
+        nc.scalar.activation(out=warm[:], in_=warm[:], func=FUNC.Sigmoid)
+
+        ident_f = const.tile([P, P], F32)
+        make_identity(nc, ident_f[:])
+
+        ident_b = const.tile([P, P], BF16)
+        nc.vector.tensor_copy(out=ident_b[:], in_=ident_f[:])
+        same_window = const.tile([P, WINDOWS], F32)
+        nc.vector.tensor_reduce(
+            out=same_window[:], in_=ident_f[:].rearrange("q (w j) -> q w j", j=PACK),
+            axis=AXIS_X, op=ALU.add,
+        )
+        gather = const.tile([P, GROUPS, M], F32)
+        nc.vector.memset(gather[:], 0.0)
+        for g in range(GROUPS):
+            nc.vector.tensor_copy(
+                out=gather[:, g, g * WINDOWS : (g + 1) * WINDOWS], in_=same_window[:]
+            )
+
+        edges_wide = const.tile([P, P], F32)
+        nc.vector.memset(edges_wide[:], 0.0)
+        nc.vector.tensor_copy(
+            out=edges_wide[0 : 2 * edge_rows, :].rearrange("r (w j) -> r w j", j=PACK),
+            in_=edges_b[:].unsqueeze(2).to_broadcast([2 * edge_rows, WINDOWS, PACK]),
+        )
+        edges_t = sum_pool.tile([P, P], F32)
+        nc.tensor.transpose(out=edges_t[:], in_=edges_wide[:], identity=ident_f[:])
+
+        def small(dtype=F32, name=None):
+            return const.tile([P, N], dtype, name=name)
+
+        def series(acc, variable, coefficients):
+            nc.vector.tensor_scalar_mul(out=acc[:], in0=variable[:], scalar1=coefficients[-1])
+            for c in reversed(coefficients[:-1]):
+                nc.vector.scalar_tensor_tensor(
+                    out=acc[:], in0=acc[:], scalar=c, in1=variable[:], op0=ALU.add, op1=ALU.mult
+                )
+
+        minus_abs = small(name="minus_abs")
+        nc.vector.scalar_tensor_tensor(
+            out=minus_abs[:], in0=kappa_b[:], scalar=-1.0, in1=kappa_b[:], op0=ALU.mult, op1=ALU.min
+        )
+        nc.vector.tensor_scalar_max(out=minus_abs[:], in0=minus_abs[:], scalar1=MOST_NEGATIVE)
+        power_i = small(I32, name="power_i")
+        nc.vector.tensor_scalar_mul(out=power_i[:], in0=minus_abs[:], scalar1=LOG2_E)
+        power = small(name="power")
+        nc.vector.tensor_copy(out=power[:], in_=power_i[:])
+        rest = small(name="rest")
+        nc.vector.scalar_tensor_tensor(
+            out=rest[:], in0=power[:], scalar=-LN2_HIGH, in1=minus_abs[:], op0=ALU.mult, op1=ALU.add
+        )
+        nc.vector.scalar_tensor_tensor(
+            out=rest[:], in0=power[:], scalar=-LN2_LOW, in1=rest[:], op0=ALU.mult, op1=ALU.add
+        )
+        two_to_power = small(I32, name="two_to_power")
+        nc.vector.tensor_scalar(
+            out=two_to_power[:], in0=power[:], scalar1=127.0, scalar2=8388608.0,
+            op0=ALU.add, op1=ALU.mult,
+        )
+        exp_series = []
+        term = 1.0
+        for d in range(1, EXP_TERMS + 1):
+            term = term / d
+            exp_series.append(term)
+        exp_rest = small(name="exp_rest")
+        series(exp_rest, rest, exp_series)
+        e = small(name="e")
+        nc.vector.scalar_tensor_tensor(
+            out=e[:], in0=exp_rest[:], scalar=1.0, in1=two_to_power[:].bitcast(F32),
+            op0=ALU.add, op1=ALU.mult,
+        )
+        z = small(name="z")
+        nc.vector.tensor_scalar_add(out=z[:], in0=e[:], scalar1=2.0)
+        nc.vector.reciprocal(out=z[:], in_=z[:])
+        nc.vector.tensor_mul(out=z[:], in0=z[:], in1=e[:])
+        z_squared = small(name="z_squared")
+        nc.vector.tensor_mul(out=z_squared[:], in0=z[:], in1=z[:])
+        atanh = small(name="atanh")
+        series(atanh, z_squared, [1.0 / (2 * i + 1) for i in range(1, ATANH_TERMS + 1)])
+        nc.vector.scalar_tensor_tensor(
+            out=atanh[:], in0=atanh[:], scalar=1.0, in1=z[:], op0=ALU.add, op1=ALU.mult
+        )
+        kappa_relu = small(name="kappa_relu")
+        nc.vector.tensor_scalar_max(out=kappa_relu[:], in0=kappa_b[:], scalar1=0.0)
+        k = small(name="k")
+        nc.vector.scalar_tensor_tensor(
+            out=k[:], in0=atanh[:], scalar=2.0, in1=kappa_relu[:], op0=ALU.mult, op1=ALU.add
+        )
+        inv_k = small(name="inv_k")
+        nc.vector.reciprocal(out=inv_k[:], in_=k[:])
+        neg_inv_k = small(name="neg_inv_k")
+        nc.vector.tensor_scalar_mul(out=neg_inv_k[:], in0=inv_k[:], scalar1=-1.0)
+
+        bias_right = const.tile([P, N, GROUPS], F32)
+        nc.vector.tensor_tensor(
+            out=bias_right[:],
+            in0=edges_t[:, 0:edge_rows].rearrange("q (n g) -> q n g", g=GROUPS),
+            in1=inv_k[:].unsqueeze(2).to_broadcast([P, N, GROUPS]),
+            op=ALU.mult,
+        )
+        bias_left = const.tile([P, N, GROUPS], F32)
+        nc.vector.tensor_tensor(
+            out=bias_left[:],
+            in0=edges_t[:, edge_rows : 2 * edge_rows].rearrange("q (n g) -> q n g", g=GROUPS),
+            in1=neg_inv_k[:].unsqueeze(2).to_broadcast([P, N, GROUPS]),
+            op=ALU.mult,
+        )
+
+        times = const.tile([P, COLS], BF16)
+
+        def every_fourth(r):
+            return shifted[r][:].rearrange("q (i j) -> q i j", j=PACK)[:, :, 0]
+
+        for r in range(STEP_COLS // SHIFT_COLS):
+            nc.scalar.copy(out=times[:, r * SHIFT_COLS : (r + 1) * SHIFT_COLS], in_=every_fourth(r))
+        load_shifted(2)
+        load_shifted(3)
+        load_x(2)
+        load_x(3)
+
+        x_grouped = {}
+        x_q = {}
+
+        def regroup_x(half):
+            grouped = xg_pool.tile([P, HALF_PASSES, B, F, PACK], BF16, align_bytes=64)
+            for b in range(B):
+                nc.vector.tensor_copy(
+                    out=grouped[:, :, b].rearrange("p c (r i) j -> p c r j i", i=4),
+                    in_=x_raw[half][:, b].rearrange("p c (j r i) -> p c r j i", j=PACK, i=4),
+                )
+            x_grouped[half] = grouped
+
+        def quantise(pool, grouped_flat):
+            codes = pool.tile([P, HALF_WORDS], U32, align_bytes=64)
+            scales = pool.tile([P, HALF_WORDS], U8, align_bytes=64)
+            nc.vector.quantize_mx(out=codes[:].bitcast(FP8X4), scales=scales[:], in_=grouped_flat)
+            return codes, scales
+
+        def quantise_x(half):
+            x_q[half] = quantise(xq_pool, x_grouped[half][:].rearrange("p c b f j -> p (c b f j)"))
+
+        sigmoids = {}
+        alpha_t = {}
+        partial = const.tile([P, N, BLOCKS_PER_N, GROUPS], F32)
+
+        def sigmoid_pair(step):
+            block, g = divmod(step, GROUPS)
+            n, part = divmod(block, BLOCKS_PER_N)
+            cols = slice(part * STEP_COLS, (part + 1) * STEP_COLS)
+            fall = sig_pool.tile([P, STEP_COLS], F32)
+            nc.scalar.activation(
+                out=fall[:], in_=times[:, cols], func=FUNC.Sigmoid,
+                bias=bias_right[:, n, g : g + 1], scale=neg_inv_k[:, n : n + 1],
+            )
+            rise = sig_pool.tile([P, STEP_COLS], F32)
+            nc.scalar.activation(
+                out=rise[:], in_=times[:, cols], func=FUNC.Sigmoid,
+                bias=bias_left[:, n, g : g + 1], scale=inv_k[:, n : n + 1],
+            )
+            sigmoids[step] = (fall, rise)
+
+        def product(step):
+            block, g = divmod(step, GROUPS)
+            n, part = divmod(block, BLOCKS_PER_N)
+            if g == 0:
+                windows_by_time = at_pool.tile([P, GROUPS, STEP_COLS], BF16)
+                alpha_t[block] = windows_by_time
+            fall, rise = sigmoids[step]
+            nc.vector.scalar_tensor_tensor(
+                out=alpha_t[block][:, g, :], in0=fall[:], scalar=1.0, in1=rise[:],
+                op0=ALU.mult, op1=ALU.mult, accum_out=partial[:, n, part, g : g + 1],
+            )
+
+        banks = {}
+
+        def transpose_pair(pair):
+            block, quarter = divmod(pair, GROUPS)
+            for side in range(2):
+                bank = bank_pool.tile([P, BANK_PASSES, M * PACK], BF16)
+                for c in range(BANK_PASSES):
+                    col = (quarter * PAIR_PASSES + side * BANK_PASSES + c) * P
+                    for g in range(GROUPS):
+                        nc.tensor.transpose(
+                            out=bank[:, c, g * P : (g + 1) * P],
+                            in_=alpha_t[block][:, g, col : col + P],
+                            identity=ident_b[:],
+                        )
+                banks[(pair, side)] = bank
+
+        alpha_grouped = {}
+        alpha_q = {}
+
+        def empty_pair(pair):
+            half, second = divmod(pair, 2)
+            if second == 0:
+                grouped = ag_pool.tile([P, 4 * BANK_COLS], BF16, align_bytes=64)
+                alpha_grouped[half] = grouped
+            for side in range(2):
+                col = (2 * second + side) * BANK_COLS
+                dst = alpha_grouped[half][:, col : col + BANK_COLS]
+                src = banks[(pair, side)][:].rearrange("p c w -> p (c w)")
+                bank_of_block = 2 * (pair % GROUPS) + side
+                if bank_of_block < 2 * GROUPS - VECTOR_BANKS:
+                    nc.scalar.copy(out=dst, in_=src)
+                else:
+                    nc.vector.tensor_copy(out=dst, in_=src)
+
+        def quantise_alpha(half):
+            alpha_q[half] = quantise(aq_pool, alpha_grouped[half][:])
+
+        numerators = {}
+
+        def multiply(half):
+            n, part = divmod(half, HALVES_PER_N)
+            quad, place = divmod(n, QUAD)
+            if place == 0 and part == 0:
+                numerator = sum_pool.tile([P, QUAD, B * F], F32, name="numerator%d" % quad)
+                numerators[quad] = numerator
+            a_codes, a_scales = alpha_q[half]
+            x_codes, x_scales = x_q[half]
+            for c in range(HALF_PASSES):
+                words = slice(c * P, (c + 1) * P)
+                nc.tensor.matmul_mx(
+                    out=numerators[quad][:, place, :],
+                    lhsT=a_codes[:, words].bitcast(FP8X4),
+                    lhsT_scale=a_scales[:, words],
+                    rhs=x_codes[:, words].bitcast(FP8X4),
+                    rhs_scale=x_scales[:, words],
+                    start=(part == 0 and c == 0),
+                    stop=(part == HALVES_PER_N - 1 and c == HALF_PASSES - 1),
+                )
+
+        inv_den = const.tile([P, N], F32)
+
+        def invert_denominators(quad):
+            channels = slice(QUAD * quad, QUAD * (quad + 1))
+            by_group = const.tile([P, GROUPS, QUAD], F32, name="by_group%d" % quad)
+            nc.vector.tensor_reduce(
+                out=by_group[:], in_=partial[:, channels].rearrange("q n h g -> q g n h"),
+                axis=AXIS_X, op=ALU.add,
+            )
+            denominator = sum_pool.tile([P, QUAD], F32)
+            for g in range(GROUPS):
+                nc.tensor.matmul(
+                    out=denominator[:], lhsT=gather[:, g, :], rhs=by_group[:, g, :],
+                    start=(g == 0), stop=(g == GROUPS - 1),
+                )
+            nc.vector.tensor_scalar_add(out=inv_den[:, channels], in0=denominator[:], scalar1=EPS)
+            nc.vector.reciprocal(out=inv_den[:, channels], in_=inv_den[:, channels])
+
+        def divide_and_store(quad):
+            channels = slice(QUAD * quad, QUAD * (quad + 1))
+            result = const.tile([P, QUAD, B, F], F32, name="result%d" % quad)
+            nc.vector.tensor_tensor(
+                out=result[:].rearrange("m n b f -> m n (b f)"),
+                in0=numerators[quad][:],
+                in1=inv_den[:, channels].unsqueeze(2).to_broadcast([P, QUAD, B * F]),
+                op=ALU.mult,
+            )
+            for b in range(B):
+                nc.sync.dma_start(
+                    out=out[b, channels].rearrange("n m f -> m n f"), in_=result[:, :, b, :]
+                )
+
+        for half in range(X_LEAD):
+            regroup_x(half)
+            load_x(half + X_LOADS_AHEAD)
+            quantise_x(half)
+
+        steps_per_quad = STEPS * QUAD // N
+        for step in range(STEPS + MULTIPLY_LAG - 1):
+            if step < STEPS:
+                sigmoid_pair(step)
+            if step % 2 == 0 and 0 <= step - MULTIPLY_LAG < STEPS:
+                multiply((step - MULTIPLY_LAG) // 2)
+            if 0 <= step - TRANSPOSE_LAG < STEPS:
+                transpose_pair(step - TRANSPOSE_LAG)
+            if 0 <= step - EMPTY_LAG < STEPS:
+                empty_pair(step - EMPTY_LAG)
+            if step % 2 == 1 and 0 <= step - QUANTISE_LAG < STEPS:
+                quantise_alpha((step - QUANTISE_LAG) // 2)
+            x_half = step // 2 + X_LEAD
+            if x_half < HALVES:
+                if step % 2 == 0:
+                    regroup_x(x_half)
+                    if x_half + X_LOADS_AHEAD < HALVES:
+                        load_x(x_half + X_LOADS_AHEAD)
+                else:
+                    quantise_x(x_half)
+            if step < STEPS:
+                product(step)
+                if (step + 1) % steps_per_quad == 0:
+                    invert_denominators(step // steps_per_quad)
+            if step >= MULTIPLY_LAG and (step - MULTIPLY_LAG + 2) % steps_per_quad == 0:
+                divide_and_store((step - MULTIPLY_LAG) // steps_per_quad)
+            r = step + STEP_COLS // SHIFT_COLS
+            if r < COLS // SHIFT_COLS:
+                nc.vector.tensor_copy(
+                    out=times[:, r * SHIFT_COLS : (r + 1) * SHIFT_COLS], in_=every_fourth(r)
+                )

@@ -42,7 +42,7 @@ HALVES = N * L // (PASS_TIMES * HALF_PASSES)
 HALVES_PER_N = HALVES // N
 HALF_WORDS = HALF_PASSES * P
 QUAD = 4
-VECTOR_BANKS = 3
+VECTOR_BANKS = 2
 X_LEAD = 1
 X_LOADS_AHEAD = 4
 SHIFT_COLS = 1024

@@ -22,7 +22,7 @@ LN2_HIGH = 0.693145751953125
 LN2_LOW = LN2 - LN2_HIGH
 LOG2_E = 1.4426950408889634
 EXP_TERMS = 12
-ATANH_TERMS = 9
+ATANH_TERMS = 7
 MOST_NEGATIVE = -80.0
 
 P = 128
@@ -31,26 +31,21 @@ PASS_TIMES = P * PACK
 WINDOWS = P // PACK
 GROUPS = M // WINDOWS
 COLS = L // PACK
-STEP_COLS = 2048
-BLOCKS_PER_N = COLS // STEP_COLS
-STEPS = N * BLOCKS_PER_N * GROUPS
+BLOCK_COLS = 2048
+TAPER_COLS = 1024
 BANK_PASSES = 2
 BANK_COLS = BANK_PASSES * M * PACK
 PAIR_PASSES = 2 * BANK_PASSES
+PAIR_COLS = PAIR_PASSES * P
+PAIRS_PER_N = COLS // PAIR_COLS
 HALF_PASSES = 2 * PAIR_PASSES
-HALVES = N * L // (PASS_TIMES * HALF_PASSES)
-HALVES_PER_N = HALVES // N
-HALF_WORDS = HALF_PASSES * P
+HALVES_PER_N = L // (PASS_TIMES * HALF_PASSES)
+HALVES = N * HALVES_PER_N
 QUAD = 4
-VECTOR_BANKS = 2
+SCALAR_BOTH = 4
 X_LEAD = 1
 X_LOADS_AHEAD = 4
 SHIFT_COLS = 1024
-
-TRANSPOSE_LAG = GROUPS
-EMPTY_LAG = TRANSPOSE_LAG + 1
-QUANTISE_LAG = EMPTY_LAG + 2
-MULTIPLY_LAG = QUANTISE_LAG + 1
 
 
 def tile_weightedaggregation_k_kernel(tc, x_aug, t, t_left, t_right, kappa, out):
@@ -61,12 +56,12 @@ def tile_weightedaggregation_k_kernel(tc, x_aug, t, t_left, t_right, kappa, out)
         shift_pool = ctx.enter_context(tc.tile_pool(name="shift", bufs=2))
         sig_pool = ctx.enter_context(tc.tile_pool(name="sig", bufs=3))
         at_pool = ctx.enter_context(tc.tile_pool(name="alpha_t", bufs=2))
-        ag_pool = ctx.enter_context(tc.tile_pool(name="alpha_grouped", bufs=2))
+        ag_pool = ctx.enter_context(tc.tile_pool(name="alpha_grouped", bufs=3))
         aq_pool = ctx.enter_context(tc.tile_pool(name="alpha_q", bufs=3))
         xr_pool = ctx.enter_context(tc.tile_pool(name="x_raw", bufs=X_LOADS_AHEAD))
         xg_pool = ctx.enter_context(tc.tile_pool(name="x_grouped", bufs=2))
         xq_pool = ctx.enter_context(tc.tile_pool(name="x_q", bufs=X_LEAD + 4))
-        bank_pool = ctx.enter_context(tc.psum_pool(name="banks", bufs=4))
+        bank_pool = ctx.enter_context(tc.psum_pool(name="banks", bufs=5))
         sum_pool = ctx.enter_context(tc.psum_pool(name="sums", bufs=1))
 
         t_flat = t.rearrange("l o -> (l o)")
@@ -100,10 +95,10 @@ def tile_weightedaggregation_k_kernel(tc, x_aug, t, t_left, t_right, kappa, out)
         nc.scalar.dma_start(out=kappa_b[:], in_=kappa.rearrange("n o -> (n o)").partition_broadcast(P))
         edge_rows = N * GROUPS
         edges_b = const.tile([2 * edge_rows, WINDOWS], BF16)
-        nc.scalar.dma_start(
+        nc.sync.dma_start(
             out=edges_b[0:edge_rows, :], in_=t_right.rearrange("n (g w) -> (n g) w", w=WINDOWS)
         )
-        nc.scalar.dma_start(
+        nc.sync.dma_start(
             out=edges_b[edge_rows : 2 * edge_rows, :],
             in_=t_left.rearrange("n (g w) -> (n g) w", w=WINDOWS),
         )
@@ -119,27 +114,13 @@ def tile_weightedaggregation_k_kernel(tc, x_aug, t, t_left, t_right, kappa, out)
         ident_f = const.tile([P, P], F32)
         make_identity(nc, ident_f[:])
 
-        ident_b = const.tile([P, P], BF16)
-        nc.vector.tensor_copy(out=ident_b[:], in_=ident_f[:])
-        same_window = const.tile([P, WINDOWS], F32)
-        nc.vector.tensor_reduce(
-            out=same_window[:], in_=ident_f[:].rearrange("q (w j) -> q w j", j=PACK),
-            axis=AXIS_X, op=ALU.add,
-        )
-        gather = const.tile([P, GROUPS, M], F32)
-        nc.vector.memset(gather[:], 0.0)
-        for g in range(GROUPS):
-            nc.vector.tensor_copy(
-                out=gather[:, g, g * WINDOWS : (g + 1) * WINDOWS], in_=same_window[:]
-            )
-
         edges_wide = const.tile([P, P], F32)
         nc.vector.memset(edges_wide[:], 0.0)
         nc.vector.tensor_copy(
             out=edges_wide[0 : 2 * edge_rows, :].rearrange("r (w j) -> r w j", j=PACK),
             in_=edges_b[:].unsqueeze(2).to_broadcast([2 * edge_rows, WINDOWS, PACK]),
         )
-        edges_t = sum_pool.tile([P, P], F32)
+        edges_t = sum_pool.tile([P, P], F32, tag="small")
         nc.tensor.transpose(out=edges_t[:], in_=edges_wide[:], identity=ident_f[:])
 
         def small(dtype=F32, name=None):
@@ -227,12 +208,26 @@ def tile_weightedaggregation_k_kernel(tc, x_aug, t, t_left, t_right, kappa, out)
         def every_fourth(r):
             return shifted[r][:].rearrange("q (i j) -> q i j", j=PACK)[:, :, 0]
 
-        for r in range(STEP_COLS // SHIFT_COLS):
+        for r in range(BLOCK_COLS // SHIFT_COLS):
             nc.scalar.copy(out=times[:, r * SHIFT_COLS : (r + 1) * SHIFT_COLS], in_=every_fourth(r))
         load_shifted(2)
         load_shifted(3)
         load_x(2)
         load_x(3)
+
+        ident_b = const.tile([P, P], BF16)
+        nc.vector.tensor_copy(out=ident_b[:], in_=ident_f[:])
+        same_window = const.tile([P, WINDOWS], F32)
+        nc.vector.tensor_reduce(
+            out=same_window[:], in_=ident_f[:].rearrange("q (w j) -> q w j", j=PACK),
+            axis=AXIS_X, op=ALU.add,
+        )
+        gather = const.tile([P, GROUPS, M], F32)
+        nc.vector.memset(gather[:], 0.0)
+        for g in range(GROUPS):
+            nc.vector.tensor_copy(
+                out=gather[:, g, g * WINDOWS : (g + 1) * WINDOWS], in_=same_window[:]
+            )
 
         x_grouped = {}
         x_q = {}
@@ -246,55 +241,75 @@ def tile_weightedaggregation_k_kernel(tc, x_aug, t, t_left, t_right, kappa, out)
                 )
             x_grouped[half] = grouped
 
-        def quantise(pool, grouped_flat):
-            codes = pool.tile([P, HALF_WORDS], U32, align_bytes=64)
-            scales = pool.tile([P, HALF_WORDS], U8, align_bytes=64)
+        def quantise(pool, grouped_flat, words):
+            codes = pool.tile([P, words], U32, align_bytes=64)
+            scales = pool.tile([P, words], U8, align_bytes=64)
             nc.vector.quantize_mx(out=codes[:].bitcast(FP8X4), scales=scales[:], in_=grouped_flat)
             return codes, scales
 
         def quantise_x(half):
-            x_q[half] = quantise(xq_pool, x_grouped[half][:].rearrange("p c b f j -> p (c b f j)"))
+            flat = x_grouped[half][:].rearrange("p c b f j -> p (c b f j)")
+            x_q[half] = quantise(xq_pool, flat, HALF_PASSES * P)
+
+        blocks = []
+        for n in range(N):
+            for first in range(0, COLS, BLOCK_COLS):
+                very_last = n == N - 1 and first + BLOCK_COLS == COLS
+                width = TAPER_COLS if very_last else BLOCK_COLS
+                for start in range(first, first + BLOCK_COLS, width):
+                    blocks.append((n, start, width))
+        steps = []
+        pairs = []
+        due = {}
+        for block in range(len(blocks)):
+            for g in range(GROUPS):
+                steps.append((block, g))
+            for col in range(0, blocks[block][2], PAIR_COLS):
+                due[len(steps) + col // PAIR_COLS] = len(pairs)
+                pairs.append((block, col))
 
         sigmoids = {}
         alpha_t = {}
-        partial = const.tile([P, N, BLOCKS_PER_N, GROUPS], F32)
+        partial = const.tile([P, N, GROUPS, COLS // TAPER_COLS], F32)
+        nc.vector.memset(partial[:], 0.0)
 
         def sigmoid_pair(step):
-            block, g = divmod(step, GROUPS)
-            n, part = divmod(block, BLOCKS_PER_N)
-            cols = slice(part * STEP_COLS, (part + 1) * STEP_COLS)
-            fall = sig_pool.tile([P, STEP_COLS], F32)
+            block, g = steps[step]
+            n, start, width = blocks[block]
+            fall = sig_pool.tile([P, BLOCK_COLS], F32)
             nc.scalar.activation(
-                out=fall[:], in_=times[:, cols], func=FUNC.Sigmoid,
+                out=fall[:, 0:width], in_=times[:, start : start + width], func=FUNC.Sigmoid,
                 bias=bias_right[:, n, g : g + 1], scale=neg_inv_k[:, n : n + 1],
             )
-            rise = sig_pool.tile([P, STEP_COLS], F32)
+            rise = sig_pool.tile([P, BLOCK_COLS], F32)
             nc.scalar.activation(
-                out=rise[:], in_=times[:, cols], func=FUNC.Sigmoid,
+                out=rise[:, 0:width], in_=times[:, start : start + width], func=FUNC.Sigmoid,
                 bias=bias_left[:, n, g : g + 1], scale=inv_k[:, n : n + 1],
             )
             sigmoids[step] = (fall, rise)
 
         def product(step):
-            block, g = divmod(step, GROUPS)
-            n, part = divmod(block, BLOCKS_PER_N)
+            block, g = steps[step]
+            n, start, width = blocks[block]
             if g == 0:
-                windows_by_time = at_pool.tile([P, GROUPS, STEP_COLS], BF16)
+                windows_by_time = at_pool.tile([P, GROUPS, BLOCK_COLS], BF16)
                 alpha_t[block] = windows_by_time
             fall, rise = sigmoids[step]
+            place = start // TAPER_COLS
             nc.vector.scalar_tensor_tensor(
-                out=alpha_t[block][:, g, :], in0=fall[:], scalar=1.0, in1=rise[:],
-                op0=ALU.mult, op1=ALU.mult, accum_out=partial[:, n, part, g : g + 1],
+                out=alpha_t[block][:, g, 0:width], in0=fall[:, 0:width], scalar=1.0,
+                in1=rise[:, 0:width], op0=ALU.mult, op1=ALU.mult,
+                accum_out=partial[:, n, g, place : place + 1],
             )
 
         banks = {}
 
         def transpose_pair(pair):
-            block, quarter = divmod(pair, GROUPS)
+            block, first = pairs[pair]
             for side in range(2):
                 bank = bank_pool.tile([P, BANK_PASSES, M * PACK], BF16)
                 for c in range(BANK_PASSES):
-                    col = (quarter * PAIR_PASSES + side * BANK_PASSES + c) * P
+                    col = first + (side * BANK_PASSES + c) * P
                     for g in range(GROUPS):
                         nc.tensor.transpose(
                             out=bank[:, c, g * P : (g + 1) * P],
@@ -307,43 +322,41 @@ def tile_weightedaggregation_k_kernel(tc, x_aug, t, t_left, t_right, kappa, out)
         alpha_q = {}
 
         def empty_pair(pair):
-            half, second = divmod(pair, 2)
-            if second == 0:
-                grouped = ag_pool.tile([P, 4 * BANK_COLS], BF16, align_bytes=64)
-                alpha_grouped[half] = grouped
+            grouped = ag_pool.tile([P, 2 * BANK_COLS], BF16, align_bytes=64)
             for side in range(2):
-                col = (2 * second + side) * BANK_COLS
-                dst = alpha_grouped[half][:, col : col + BANK_COLS]
+                dst = grouped[:, side * BANK_COLS : (side + 1) * BANK_COLS]
                 src = banks[(pair, side)][:].rearrange("p c w -> p (c w)")
-                bank_of_block = 2 * (pair % GROUPS) + side
-                if bank_of_block < 2 * GROUPS - VECTOR_BANKS:
+                if side == 0 or pair % SCALAR_BOTH == 0:
                     nc.scalar.copy(out=dst, in_=src)
                 else:
                     nc.vector.tensor_copy(out=dst, in_=src)
+            alpha_grouped[pair] = grouped
 
-        def quantise_alpha(half):
-            alpha_q[half] = quantise(aq_pool, alpha_grouped[half][:])
+        def quantise_alpha(pair):
+            alpha_q[pair] = quantise(aq_pool, alpha_grouped[pair][:], PAIR_PASSES * P)
 
         numerators = {}
 
-        def multiply(half):
-            n, part = divmod(half, HALVES_PER_N)
+        def multiply(pair):
+            n, part = divmod(pair, PAIRS_PER_N)
             quad, place = divmod(n, QUAD)
             if place == 0 and part == 0:
                 numerator = sum_pool.tile([P, QUAD, B * F], F32, name="numerator%d" % quad)
                 numerators[quad] = numerator
-            a_codes, a_scales = alpha_q[half]
-            x_codes, x_scales = x_q[half]
-            for c in range(HALF_PASSES):
-                words = slice(c * P, (c + 1) * P)
+            a_codes, a_scales = alpha_q[pair]
+            x_codes, x_scales = x_q[pair // 2]
+            x_first = (pair % 2) * PAIR_PASSES
+            for c in range(PAIR_PASSES):
+                a_words = slice(c * P, (c + 1) * P)
+                x_words = slice((x_first + c) * P, (x_first + c + 1) * P)
                 nc.tensor.matmul_mx(
                     out=numerators[quad][:, place, :],
-                    lhsT=a_codes[:, words].bitcast(FP8X4),
-                    lhsT_scale=a_scales[:, words],
-                    rhs=x_codes[:, words].bitcast(FP8X4),
-                    rhs_scale=x_scales[:, words],
+                    lhsT=a_codes[:, a_words].bitcast(FP8X4),
+                    lhsT_scale=a_scales[:, a_words],
+                    rhs=x_codes[:, x_words].bitcast(FP8X4),
+                    rhs_scale=x_scales[:, x_words],
                     start=(part == 0 and c == 0),
-                    stop=(part == HALVES_PER_N - 1 and c == HALF_PASSES - 1),
+                    stop=(part == PAIRS_PER_N - 1 and c == PAIR_PASSES - 1),
                 )
 
         inv_den = const.tile([P, N], F32)
@@ -352,10 +365,10 @@ def tile_weightedaggregation_k_kernel(tc, x_aug, t, t_left, t_right, kappa, out)
             channels = slice(QUAD * quad, QUAD * (quad + 1))
             by_group = const.tile([P, GROUPS, QUAD], F32, name="by_group%d" % quad)
             nc.vector.tensor_reduce(
-                out=by_group[:], in_=partial[:, channels].rearrange("q n h g -> q g n h"),
+                out=by_group[:], in_=partial[:, channels].rearrange("q n g h -> q g n h"),
                 axis=AXIS_X, op=ALU.add,
             )
-            denominator = sum_pool.tile([P, QUAD], F32)
+            denominator = sum_pool.tile([P, QUAD], F32, tag="small")
             for g in range(GROUPS):
                 nc.tensor.matmul(
                     out=denominator[:], lhsT=gather[:, g, :], rhs=by_group[:, g, :],
@@ -383,18 +396,18 @@ def tile_weightedaggregation_k_kernel(tc, x_aug, t, t_left, t_right, kappa, out)
             load_x(half + X_LOADS_AHEAD)
             quantise_x(half)
 
-        steps_per_quad = STEPS * QUAD // N
-        for step in range(STEPS + MULTIPLY_LAG - 1):
-            if step < STEPS:
+        for step in range(max(due) + 4):
+            if step < len(steps):
                 sigmoid_pair(step)
-            if step % 2 == 0 and 0 <= step - MULTIPLY_LAG < STEPS:
-                multiply((step - MULTIPLY_LAG) // 2)
-            if 0 <= step - TRANSPOSE_LAG < STEPS:
-                transpose_pair(step - TRANSPOSE_LAG)
-            if 0 <= step - EMPTY_LAG < STEPS:
-                empty_pair(step - EMPTY_LAG)
-            if step % 2 == 1 and 0 <= step - QUANTISE_LAG < STEPS:
-                quantise_alpha((step - QUANTISE_LAG) // 2)
+            multiplied = due.get(step - 3)
+            if multiplied is not None:
+                multiply(multiplied)
+            if step in due:
+                transpose_pair(due[step])
+            if step - 1 in due:
+                empty_pair(due[step - 1])
+            if step - 2 in due:
+                quantise_alpha(due[step - 2])
             x_half = step // 2 + X_LEAD
             if x_half < HALVES:
                 if step % 2 == 0:
@@ -403,13 +416,14 @@ def tile_weightedaggregation_k_kernel(tc, x_aug, t, t_left, t_right, kappa, out)
                         load_x(x_half + X_LOADS_AHEAD)
                 else:
                     quantise_x(x_half)
-            if step < STEPS:
+            if step < len(steps):
                 product(step)
-                if (step + 1) % steps_per_quad == 0:
-                    invert_denominators(step // steps_per_quad)
-            if step >= MULTIPLY_LAG and (step - MULTIPLY_LAG + 2) % steps_per_quad == 0:
-                divide_and_store((step - MULTIPLY_LAG) // steps_per_quad)
-            r = step + STEP_COLS // SHIFT_COLS
+                n, start, width = blocks[steps[step][0]]
+                if steps[step][1] == GROUPS - 1 and start + width == COLS and (n + 1) % QUAD == 0:
+                    invert_denominators(n // QUAD)
+            if multiplied is not None and (multiplied + 1) % (QUAD * PAIRS_PER_N) == 0:
+                divide_and_store(multiplied // (QUAD * PAIRS_PER_N))
+            r = step + BLOCK_COLS // SHIFT_COLS
             if r < COLS // SHIFT_COLS:
                 nc.vector.tensor_copy(
                     out=times[:, r * SHIFT_COLS : (r + 1) * SHIFT_COLS], in_=every_fourth(r)

@@ -21,8 +21,6 @@ LN2 = 0.6931471805599453
 LN2_HIGH = 0.693145751953125
 LN2_LOW = LN2 - LN2_HIGH
 LOG2_E = 1.4426950408889634
-EXP_TERMS = 12
-ATANH_TERMS = 7
 MOST_NEGATIVE = -80.0
 
 P = 128
@@ -31,21 +29,23 @@ PASS_TIMES = P * PACK
 WINDOWS = P // PACK
 GROUPS = M // WINDOWS
 COLS = L // PACK
-BLOCK_COLS = 2048
-TAPER_COLS = 1024
 BANK_PASSES = 2
 BANK_COLS = BANK_PASSES * M * PACK
-PAIR_PASSES = 2 * BANK_PASSES
-PAIR_COLS = PAIR_PASSES * P
-PAIRS_PER_N = COLS // PAIR_COLS
-HALF_PASSES = 2 * PAIR_PASSES
-HALVES_PER_N = L // (PASS_TIMES * HALF_PASSES)
-HALVES = N * HALVES_PER_N
+BANKS = 2
+PERIOD_PASSES = BANKS * BANK_PASSES
+PERIOD_COLS = PERIOD_PASSES * P
+PERIODS_PER_N = COLS // PERIOD_COLS
+PERIODS = N * PERIODS_PER_N
+BLOCK_PERIODS = 4
+FIRST_BLOCKS = (1, 1, 2, 4)
+LAST_BLOCKS = (4, 2, 1, 1)
+BLOCK_COLS = BLOCK_PERIODS * PERIOD_COLS
+BLOCKS_PER_N = 4
 QUAD = 4
 SCALAR_BOTH = 4
-X_LEAD = 1
-X_LOADS_AHEAD = 4
-SHIFT_COLS = 1024
+X_LOADS = 6
+CHUNK_COLS = PERIOD_COLS
+CHUNKS = COLS // CHUNK_COLS
 
 
 def tile_weightedaggregation_k_kernel(tc, x_aug, t, t_left, t_right, kappa, out):
@@ -53,25 +53,25 @@ def tile_weightedaggregation_k_kernel(tc, x_aug, t, t_left, t_right, kappa, out)
     with ExitStack() as ctx:
         ctx.enter_context(tc.manual_schedule())
         const = ctx.enter_context(tc.tile_pool(name="const", bufs=1))
-        shift_pool = ctx.enter_context(tc.tile_pool(name="shift", bufs=2))
-        sig_pool = ctx.enter_context(tc.tile_pool(name="sig", bufs=3))
+        shift_pool = ctx.enter_context(tc.tile_pool(name="shift", bufs=4))
+        sig_pool = ctx.enter_context(tc.tile_pool(name="sig", bufs=4))
         at_pool = ctx.enter_context(tc.tile_pool(name="alpha_t", bufs=2))
-        ag_pool = ctx.enter_context(tc.tile_pool(name="alpha_grouped", bufs=3))
+        ag_pool = ctx.enter_context(tc.tile_pool(name="alpha_grouped", bufs=4))
         aq_pool = ctx.enter_context(tc.tile_pool(name="alpha_q", bufs=3))
-        xr_pool = ctx.enter_context(tc.tile_pool(name="x_raw", bufs=X_LOADS_AHEAD))
+        xr_pool = ctx.enter_context(tc.tile_pool(name="x_raw", bufs=X_LOADS))
         xg_pool = ctx.enter_context(tc.tile_pool(name="x_grouped", bufs=2))
-        xq_pool = ctx.enter_context(tc.tile_pool(name="x_q", bufs=X_LEAD + 4))
+        xq_pool = ctx.enter_context(tc.tile_pool(name="x_q", bufs=13))
         bank_pool = ctx.enter_context(tc.psum_pool(name="banks", bufs=5))
         sum_pool = ctx.enter_context(tc.psum_pool(name="sums", bufs=1))
 
         t_flat = t.rearrange("l o -> (l o)")
-        shift_run = PACK * (SHIFT_COLS - 1) + 1
+        shift_run = PACK * (CHUNK_COLS - 1) + 1
         shifted = {}
 
         def load_shifted(r):
-            run = shift_pool.tile([P, PACK * SHIFT_COLS], BF16)
+            run = shift_pool.tile([P, PACK * CHUNK_COLS], BF16)
             for j in range(PACK):
-                start = PACK * SHIFT_COLS * r + j
+                start = PACK * CHUNK_COLS * r + j
                 nc.sync.dma_start(
                     out=run[j:P:PACK, 0:shift_run],
                     in_=t_flat[start : start + shift_run].partition_broadcast(WINDOWS),
@@ -80,21 +80,25 @@ def tile_weightedaggregation_k_kernel(tc, x_aug, t, t_left, t_right, kappa, out)
 
         x_raw = {}
 
-        def load_x(half):
-            n, part = divmod(half, HALVES_PER_N)
-            rows = slice(part * HALF_PASSES * PASS_TIMES, (part + 1) * HALF_PASSES * PASS_TIMES)
-            raw = xr_pool.tile([P, B, HALF_PASSES, PACK * F], BF16)
+        def load_x(period):
+            if period >= PERIODS:
+                return
+            n, part = divmod(period, PERIODS_PER_N)
+            span = PERIOD_PASSES * PASS_TIMES
+            rows = slice(part * span, (part + 1) * span)
+            raw = xr_pool.tile([P, PERIOD_PASSES, B, PACK * F], BF16)
             for b in range(B):
                 nc.sync.dma_start(
-                    out=raw[:, b],
+                    out=raw[:, :, b],
                     in_=x_aug[b, n, rows, :].rearrange("(c p j) f -> p c (j f)", p=P, j=PACK),
                 )
-            x_raw[half] = raw
+            x_raw[period] = raw
 
         kappa_b = const.tile([P, N], BF16)
         nc.scalar.dma_start(out=kappa_b[:], in_=kappa.rearrange("n o -> (n o)").partition_broadcast(P))
         edge_rows = N * GROUPS
         edges_b = const.tile([2 * edge_rows, WINDOWS], BF16)
+        load_shifted(0)
         nc.sync.dma_start(
             out=edges_b[0:edge_rows, :], in_=t_right.rearrange("n (g w) -> (n g) w", w=WINDOWS)
         )
@@ -102,9 +106,10 @@ def tile_weightedaggregation_k_kernel(tc, x_aug, t, t_left, t_right, kappa, out)
             out=edges_b[edge_rows : 2 * edge_rows, :],
             in_=t_left.rearrange("n (g w) -> (n g) w", w=WINDOWS),
         )
-        load_shifted(0)
         load_shifted(1)
         load_x(0)
+        load_shifted(2)
+        load_shifted(3)
         load_x(1)
 
         warm = const.tile([P, 1], F32)
@@ -114,6 +119,83 @@ def tile_weightedaggregation_k_kernel(tc, x_aug, t, t_left, t_right, kappa, out)
         ident_f = const.tile([P, P], F32)
         make_identity(nc, ident_f[:])
 
+        def small(name, dtype=F32):
+            return const.tile([P, N], dtype, name=name)
+
+        def add_mult(out, in0, scalar, in1):
+            nc.vector.scalar_tensor_tensor(
+                out=out[:], in0=in0[:], scalar=scalar, in1=in1[:], op0=ALU.add, op1=ALU.mult
+            )
+
+        minus_abs = small("minus_abs")
+        nc.vector.scalar_tensor_tensor(
+            out=minus_abs[:], in0=kappa_b[:], scalar=-1.0, in1=kappa_b[:], op0=ALU.mult, op1=ALU.min
+        )
+        kappa_relu = small("kappa_relu")
+        nc.vector.tensor_scalar_max(out=kappa_relu[:], in0=kappa_b[:], scalar1=0.0)
+        nc.vector.tensor_scalar_max(out=minus_abs[:], in0=minus_abs[:], scalar1=MOST_NEGATIVE)
+        power_i = small("power_i", I32)
+        nc.vector.tensor_scalar_mul(out=power_i[:], in0=minus_abs[:], scalar1=LOG2_E)
+        power = small("power")
+        nc.vector.tensor_copy(out=power[:], in_=power_i[:])
+        r = small("r")
+        nc.vector.scalar_tensor_tensor(
+            out=r[:], in0=power[:], scalar=-LN2_HIGH, in1=minus_abs[:], op0=ALU.mult, op1=ALU.add
+        )
+        two_to_power = small("two_to_power", I32)
+        nc.vector.tensor_scalar(
+            out=two_to_power[:], in0=power[:], scalar1=127.0, scalar2=8388608.0,
+            op0=ALU.add, op1=ALU.mult,
+        )
+        nc.vector.scalar_tensor_tensor(
+            out=r[:], in0=power[:], scalar=-LN2_LOW, in1=r[:], op0=ALU.mult, op1=ALU.add
+        )
+        r2 = small("r2")
+        nc.vector.tensor_mul(out=r2[:], in0=r[:], in1=r[:])
+        r_30th = small("r_30th")
+        nc.vector.tensor_scalar_mul(out=r_30th[:], in0=r[:], scalar1=1.0 / 30.0)
+        odd = small("odd")
+        add_mult(odd, r2, 420.0, r2)
+        even = small("even")
+        add_mult(even, r2, 112.0, r2)
+        add_mult(odd, odd, 15120.0, r_30th)
+        e_num = small("e_num")
+        nc.vector.scalar_tensor_tensor(
+            out=e_num[:], in0=even[:], scalar=1008.0, in1=odd[:], op0=ALU.add, op1=ALU.add
+        )
+        e_den = small("e_den")
+        nc.vector.scalar_tensor_tensor(
+            out=e_den[:], in0=even[:], scalar=1008.0, in1=odd[:], op0=ALU.add, op1=ALU.subtract
+        )
+        nc.vector.tensor_mul(out=e_num[:], in0=e_num[:], in1=two_to_power[:].bitcast(F32))
+        z = small("z")
+        nc.vector.scalar_tensor_tensor(
+            out=z[:], in0=e_den[:], scalar=2.0, in1=e_num[:], op0=ALU.mult, op1=ALU.add
+        )
+        nc.vector.reciprocal(out=z[:], in_=z[:])
+        nc.vector.tensor_mul(out=z[:], in0=z[:], in1=e_num[:])
+        y = small("y")
+        nc.vector.tensor_mul(out=y[:], in0=z[:], in1=z[:])
+        top = small("top")
+        nc.vector.tensor_scalar_mul(out=top[:], in0=y[:], scalar1=-256.0)
+        bottom = small("bottom")
+        nc.vector.tensor_scalar_mul(out=bottom[:], in0=y[:], scalar1=-1225.0)
+        add_mult(top, top, 5943.0, y)
+        add_mult(bottom, bottom, 11025.0, y)
+        add_mult(top, top, -19250.0, y)
+        add_mult(bottom, bottom, -24255.0, y)
+        add_mult(top, top, 15015.0, z)
+        nc.vector.tensor_scalar_add(out=bottom[:], in0=bottom[:], scalar1=15015.0)
+        nc.vector.tensor_mul(out=kappa_relu[:], in0=kappa_relu[:], in1=bottom[:])
+        inv_k = small("inv_k")
+        nc.vector.scalar_tensor_tensor(
+            out=inv_k[:], in0=top[:], scalar=2.0, in1=kappa_relu[:], op0=ALU.mult, op1=ALU.add
+        )
+        nc.vector.reciprocal(out=inv_k[:], in_=inv_k[:])
+        nc.vector.tensor_mul(out=inv_k[:], in0=inv_k[:], in1=bottom[:])
+        neg_inv_k = small("neg_inv_k")
+        nc.vector.tensor_scalar_mul(out=neg_inv_k[:], in0=inv_k[:], scalar1=-1.0)
+
         edges_wide = const.tile([P, P], F32)
         nc.vector.memset(edges_wide[:], 0.0)
         nc.vector.tensor_copy(
@@ -122,71 +204,6 @@ def tile_weightedaggregation_k_kernel(tc, x_aug, t, t_left, t_right, kappa, out)
         )
         edges_t = sum_pool.tile([P, P], F32, tag="small")
         nc.tensor.transpose(out=edges_t[:], in_=edges_wide[:], identity=ident_f[:])
-
-        def small(dtype=F32, name=None):
-            return const.tile([P, N], dtype, name=name)
-
-        def series(acc, variable, coefficients):
-            nc.vector.tensor_scalar_mul(out=acc[:], in0=variable[:], scalar1=coefficients[-1])
-            for c in reversed(coefficients[:-1]):
-                nc.vector.scalar_tensor_tensor(
-                    out=acc[:], in0=acc[:], scalar=c, in1=variable[:], op0=ALU.add, op1=ALU.mult
-                )
-
-        minus_abs = small(name="minus_abs")
-        nc.vector.scalar_tensor_tensor(
-            out=minus_abs[:], in0=kappa_b[:], scalar=-1.0, in1=kappa_b[:], op0=ALU.mult, op1=ALU.min
-        )
-        nc.vector.tensor_scalar_max(out=minus_abs[:], in0=minus_abs[:], scalar1=MOST_NEGATIVE)
-        power_i = small(I32, name="power_i")
-        nc.vector.tensor_scalar_mul(out=power_i[:], in0=minus_abs[:], scalar1=LOG2_E)
-        power = small(name="power")
-        nc.vector.tensor_copy(out=power[:], in_=power_i[:])
-        rest = small(name="rest")
-        nc.vector.scalar_tensor_tensor(
-            out=rest[:], in0=power[:], scalar=-LN2_HIGH, in1=minus_abs[:], op0=ALU.mult, op1=ALU.add
-        )
-        nc.vector.scalar_tensor_tensor(
-            out=rest[:], in0=power[:], scalar=-LN2_LOW, in1=rest[:], op0=ALU.mult, op1=ALU.add
-        )
-        two_to_power = small(I32, name="two_to_power")
-        nc.vector.tensor_scalar(
-            out=two_to_power[:], in0=power[:], scalar1=127.0, scalar2=8388608.0,
-            op0=ALU.add, op1=ALU.mult,
-        )
-        exp_series = []
-        term = 1.0
-        for d in range(1, EXP_TERMS + 1):
-            term = term / d
-            exp_series.append(term)
-        exp_rest = small(name="exp_rest")
-        series(exp_rest, rest, exp_series)
-        e = small(name="e")
-        nc.vector.scalar_tensor_tensor(
-            out=e[:], in0=exp_rest[:], scalar=1.0, in1=two_to_power[:].bitcast(F32),
-            op0=ALU.add, op1=ALU.mult,
-        )
-        z = small(name="z")
-        nc.vector.tensor_scalar_add(out=z[:], in0=e[:], scalar1=2.0)
-        nc.vector.reciprocal(out=z[:], in_=z[:])
-        nc.vector.tensor_mul(out=z[:], in0=z[:], in1=e[:])
-        z_squared = small(name="z_squared")
-        nc.vector.tensor_mul(out=z_squared[:], in0=z[:], in1=z[:])
-        atanh = small(name="atanh")
-        series(atanh, z_squared, [1.0 / (2 * i + 1) for i in range(1, ATANH_TERMS + 1)])
-        nc.vector.scalar_tensor_tensor(
-            out=atanh[:], in0=atanh[:], scalar=1.0, in1=z[:], op0=ALU.add, op1=ALU.mult
-        )
-        kappa_relu = small(name="kappa_relu")
-        nc.vector.tensor_scalar_max(out=kappa_relu[:], in0=kappa_b[:], scalar1=0.0)
-        k = small(name="k")
-        nc.vector.scalar_tensor_tensor(
-            out=k[:], in0=atanh[:], scalar=2.0, in1=kappa_relu[:], op0=ALU.mult, op1=ALU.add
-        )
-        inv_k = small(name="inv_k")
-        nc.vector.reciprocal(out=inv_k[:], in_=k[:])
-        neg_inv_k = small(name="neg_inv_k")
-        nc.vector.tensor_scalar_mul(out=neg_inv_k[:], in0=inv_k[:], scalar1=-1.0)
 
         bias_right = const.tile([P, N, GROUPS], F32)
         nc.vector.tensor_tensor(
@@ -205,15 +222,16 @@ def tile_weightedaggregation_k_kernel(tc, x_aug, t, t_left, t_right, kappa, out)
 
         times = const.tile([P, COLS], BF16)
 
-        def every_fourth(r):
-            return shifted[r][:].rearrange("q (i j) -> q i j", j=PACK)[:, :, 0]
+        def fill_times(copy, r):
+            copy(
+                out=times[:, r * CHUNK_COLS : (r + 1) * CHUNK_COLS],
+                in_=shifted[r][:].rearrange("q (i j) -> q i j", j=PACK)[:, :, 0],
+            )
 
-        for r in range(BLOCK_COLS // SHIFT_COLS):
-            nc.scalar.copy(out=times[:, r * SHIFT_COLS : (r + 1) * SHIFT_COLS], in_=every_fourth(r))
-        load_shifted(2)
-        load_shifted(3)
-        load_x(2)
-        load_x(3)
+        for r in range(CHUNKS // 2):
+            fill_times(nc.scalar.copy, r)
+            load_shifted(r + CHUNKS // 2)
+            load_x(r + 2)
 
         ident_b = const.tile([P, P], BF16)
         nc.vector.tensor_copy(out=ident_b[:], in_=ident_f[:])
@@ -232,14 +250,16 @@ def tile_weightedaggregation_k_kernel(tc, x_aug, t, t_left, t_right, kappa, out)
         x_grouped = {}
         x_q = {}
 
-        def regroup_x(half):
-            grouped = xg_pool.tile([P, HALF_PASSES, B, F, PACK], BF16, align_bytes=64)
-            for b in range(B):
-                nc.vector.tensor_copy(
-                    out=grouped[:, :, b].rearrange("p c (r i) j -> p c r j i", i=4),
-                    in_=x_raw[half][:, b].rearrange("p c (j r i) -> p c r j i", j=PACK, i=4),
-                )
-            x_grouped[half] = grouped
+        def regroup_x(period):
+            if period >= PERIODS:
+                return
+            grouped = xg_pool.tile([P, PERIOD_PASSES, B, F, PACK], BF16, align_bytes=64)
+            nc.vector.tensor_copy(
+                out=grouped[:].rearrange("p c b (r i) j -> p (c b) r j i", i=4),
+                in_=x_raw[period][:].rearrange("p c b (j r i) -> p (c b) r j i", j=PACK, i=4),
+            )
+            x_grouped[period] = grouped
+            load_x(period + X_LOADS)
 
         def quantise(pool, grouped_flat, words):
             codes = pool.tile([P, words], U32, align_bytes=64)
@@ -247,66 +267,82 @@ def tile_weightedaggregation_k_kernel(tc, x_aug, t, t_left, t_right, kappa, out)
             nc.vector.quantize_mx(out=codes[:].bitcast(FP8X4), scales=scales[:], in_=grouped_flat)
             return codes, scales
 
-        def quantise_x(half):
-            flat = x_grouped[half][:].rearrange("p c b f j -> p (c b f j)")
-            x_q[half] = quantise(xq_pool, flat, HALF_PASSES * P)
+        def quantise_x(period):
+            if period < PERIODS:
+                flat = x_grouped[period][:].rearrange("p c b f j -> p (c b f j)")
+                x_q[period] = quantise(xq_pool, flat, PERIOD_PASSES * P)
 
         blocks = []
         for n in range(N):
-            for first in range(0, COLS, BLOCK_COLS):
-                very_last = n == N - 1 and first + BLOCK_COLS == COLS
-                width = TAPER_COLS if very_last else BLOCK_COLS
-                for start in range(first, first + BLOCK_COLS, width):
-                    blocks.append((n, start, width))
-        steps = []
-        pairs = []
-        due = {}
+            widths = (BLOCK_PERIODS,) * (PERIODS_PER_N // BLOCK_PERIODS)
+            if n == 0:
+                widths = FIRST_BLOCKS
+            if n == N - 1:
+                widths = LAST_BLOCKS
+            first = n * PERIODS_PER_N
+            for place in range(len(widths)):
+                blocks.append((n, place, first, widths[place]))
+                first += widths[place]
+        block_of = {}
+        slots = []
+        due = []
+        ready = []
         for block in range(len(blocks)):
-            for g in range(GROUPS):
-                steps.append((block, g))
-            for col in range(0, blocks[block][2], PAIR_COLS):
-                due[len(steps) + col // PAIR_COLS] = len(pairs)
-                pairs.append((block, col))
+            width = blocks[block][3]
+            for s in range(width):
+                share = GROUPS // width
+                slots.append([(block, g) for g in range(s * share, (s + 1) * share)])
+                last = len(slots) > PERIODS - LAST_BLOCKS[0]
+                due.append([ready.pop(0) for taken in range(min(len(ready), 2 if last else 1))])
+            for period in range(blocks[block][2], blocks[block][2] + width):
+                block_of[period] = block
+                ready.append(period)
+        while ready:
+            due.append([ready.pop(0)])
+
+        def due_in(slot):
+            return due[slot] if 0 <= slot < len(due) else []
 
         sigmoids = {}
         alpha_t = {}
-        partial = const.tile([P, N, GROUPS, COLS // TAPER_COLS], F32)
+        partial = const.tile([P, N, GROUPS, BLOCKS_PER_N], F32)
         nc.vector.memset(partial[:], 0.0)
 
-        def sigmoid_pair(step):
-            block, g = steps[step]
-            n, start, width = blocks[block]
+        def sigmoid_pair(block, g):
+            n, place, first, width = blocks[block]
+            start = (first - n * PERIODS_PER_N) * PERIOD_COLS
+            cols = width * PERIOD_COLS
             fall = sig_pool.tile([P, BLOCK_COLS], F32)
             nc.scalar.activation(
-                out=fall[:, 0:width], in_=times[:, start : start + width], func=FUNC.Sigmoid,
+                out=fall[:, 0:cols], in_=times[:, start : start + cols], func=FUNC.Sigmoid,
                 bias=bias_right[:, n, g : g + 1], scale=neg_inv_k[:, n : n + 1],
             )
             rise = sig_pool.tile([P, BLOCK_COLS], F32)
             nc.scalar.activation(
-                out=rise[:, 0:width], in_=times[:, start : start + width], func=FUNC.Sigmoid,
+                out=rise[:, 0:cols], in_=times[:, start : start + cols], func=FUNC.Sigmoid,
                 bias=bias_left[:, n, g : g + 1], scale=inv_k[:, n : n + 1],
             )
-            sigmoids[step] = (fall, rise)
+            sigmoids[(block, g)] = (fall, rise)
 
-        def product(step):
-            block, g = steps[step]
-            n, start, width = blocks[block]
+        def product(block, g):
+            n, place, first, width = blocks[block]
+            cols = width * PERIOD_COLS
             if g == 0:
                 windows_by_time = at_pool.tile([P, GROUPS, BLOCK_COLS], BF16)
                 alpha_t[block] = windows_by_time
-            fall, rise = sigmoids[step]
-            place = start // TAPER_COLS
+            fall, rise = sigmoids[(block, g)]
             nc.vector.scalar_tensor_tensor(
-                out=alpha_t[block][:, g, 0:width], in0=fall[:, 0:width], scalar=1.0,
-                in1=rise[:, 0:width], op0=ALU.mult, op1=ALU.mult,
+                out=alpha_t[block][:, g, 0:cols], in0=fall[:, 0:cols], scalar=1.0,
+                in1=rise[:, 0:cols], op0=ALU.mult, op1=ALU.mult,
                 accum_out=partial[:, n, g, place : place + 1],
             )
 
         banks = {}
 
-        def transpose_pair(pair):
-            block, first = pairs[pair]
-            for side in range(2):
+        def transpose(period):
+            block = block_of[period]
+            first = (period - blocks[block][2]) * PERIOD_COLS
+            for side in range(BANKS):
                 bank = bank_pool.tile([P, BANK_PASSES, M * PACK], BF16)
                 for c in range(BANK_PASSES):
                     col = first + (side * BANK_PASSES + c) * P
@@ -316,47 +352,45 @@ def tile_weightedaggregation_k_kernel(tc, x_aug, t, t_left, t_right, kappa, out)
                             in_=alpha_t[block][:, g, col : col + P],
                             identity=ident_b[:],
                         )
-                banks[(pair, side)] = bank
+                banks[(period, side)] = bank
 
         alpha_grouped = {}
         alpha_q = {}
 
-        def empty_pair(pair):
-            grouped = ag_pool.tile([P, 2 * BANK_COLS], BF16, align_bytes=64)
-            for side in range(2):
+        def empty_banks(period):
+            grouped = ag_pool.tile([P, BANKS * BANK_COLS], BF16, align_bytes=64)
+            for side in range(BANKS):
                 dst = grouped[:, side * BANK_COLS : (side + 1) * BANK_COLS]
-                src = banks[(pair, side)][:].rearrange("p c w -> p (c w)")
-                if side == 0 or pair % SCALAR_BOTH == 0:
+                src = banks[(period, side)][:].rearrange("p c w -> p (c w)")
+                if side == 0 or period % SCALAR_BOTH == 0:
                     nc.scalar.copy(out=dst, in_=src)
                 else:
                     nc.vector.tensor_copy(out=dst, in_=src)
-            alpha_grouped[pair] = grouped
+            alpha_grouped[period] = grouped
 
-        def quantise_alpha(pair):
-            alpha_q[pair] = quantise(aq_pool, alpha_grouped[pair][:], PAIR_PASSES * P)
+        def quantise_alpha(period):
+            alpha_q[period] = quantise(aq_pool, alpha_grouped[period][:], PERIOD_PASSES * P)
 
         numerators = {}
 
-        def multiply(pair):
-            n, part = divmod(pair, PAIRS_PER_N)
+        def multiply(period):
+            n, part = divmod(period, PERIODS_PER_N)
             quad, place = divmod(n, QUAD)
             if place == 0 and part == 0:
                 numerator = sum_pool.tile([P, QUAD, B * F], F32, name="numerator%d" % quad)
                 numerators[quad] = numerator
-            a_codes, a_scales = alpha_q[pair]
-            x_codes, x_scales = x_q[pair // 2]
-            x_first = (pair % 2) * PAIR_PASSES
-            for c in range(PAIR_PASSES):
-                a_words = slice(c * P, (c + 1) * P)
-                x_words = slice((x_first + c) * P, (x_first + c + 1) * P)
+            a_codes, a_scales = alpha_q[period]
+            x_codes, x_scales = x_q[period]
+            for c in range(PERIOD_PASSES):
+                words = slice(c * P, (c + 1) * P)
                 nc.tensor.matmul_mx(
                     out=numerators[quad][:, place, :],
-                    lhsT=a_codes[:, a_words].bitcast(FP8X4),
-                    lhsT_scale=a_scales[:, a_words],
-                    rhs=x_codes[:, x_words].bitcast(FP8X4),
-                    rhs_scale=x_scales[:, x_words],
+                    lhsT=a_codes[:, words].bitcast(FP8X4),
+                    lhsT_scale=a_scales[:, words],
+                    rhs=x_codes[:, words].bitcast(FP8X4),
+                    rhs_scale=x_scales[:, words],
                     start=(part == 0 and c == 0),
-                    stop=(part == PAIRS_PER_N - 1 and c == PAIR_PASSES - 1),
+                    stop=(part == PERIODS_PER_N - 1 and c == PERIOD_PASSES - 1),
                 )
 
         inv_den = const.tile([P, N], F32)
@@ -391,40 +425,33 @@ def tile_weightedaggregation_k_kernel(tc, x_aug, t, t_left, t_right, kappa, out)
                     out=out[b, channels].rearrange("n m f -> m n f"), in_=result[:, :, b, :]
                 )
 
-        for half in range(X_LEAD):
-            regroup_x(half)
-            load_x(half + X_LOADS_AHEAD)
-            quantise_x(half)
-
-        for step in range(max(due) + 4):
-            if step < len(steps):
-                sigmoid_pair(step)
-            multiplied = due.get(step - 3)
-            if multiplied is not None:
-                multiply(multiplied)
-            if step in due:
-                transpose_pair(due[step])
-            if step - 1 in due:
-                empty_pair(due[step - 1])
-            if step - 2 in due:
-                quantise_alpha(due[step - 2])
-            x_half = step // 2 + X_LEAD
-            if x_half < HALVES:
-                if step % 2 == 0:
-                    regroup_x(x_half)
-                    if x_half + X_LOADS_AHEAD < HALVES:
-                        load_x(x_half + X_LOADS_AHEAD)
-                else:
-                    quantise_x(x_half)
-            if step < len(steps):
-                product(step)
-                n, start, width = blocks[steps[step][0]]
-                if steps[step][1] == GROUPS - 1 and start + width == COLS and (n + 1) % QUAD == 0:
-                    invert_denominators(n // QUAD)
-            if multiplied is not None and (multiplied + 1) % (QUAD * PAIRS_PER_N) == 0:
-                divide_and_store(multiplied // (QUAD * PAIRS_PER_N))
-            r = step + BLOCK_COLS // SHIFT_COLS
-            if r < COLS // SHIFT_COLS:
-                nc.vector.tensor_copy(
-                    out=times[:, r * SHIFT_COLS : (r + 1) * SHIFT_COLS], in_=every_fourth(r)
-                )
+        x_regrouped = 0
+        x_quantised = 0
+        for slot in range(len(due) + 3):
+            work = slots[slot] if slot < len(slots) else []
+            for block, g in work:
+                sigmoid_pair(block, g)
+            for period in due_in(slot - 3):
+                multiply(period)
+            for period in due_in(slot - 1):
+                empty_banks(period)
+            for period in due_in(slot):
+                transpose(period)
+            for period in due_in(slot - 2):
+                quantise_alpha(period)
+            for turn in range(1 if due_in(slot - 1) else 2):
+                if x_quantised < x_regrouped:
+                    quantise_x(x_quantised)
+                    x_quantised += 1
+                if x_regrouped < PERIODS:
+                    regroup_x(x_regrouped)
+                    x_regrouped += 1
+            for block, g in work:
+                product(block, g)
+            if slot < CHUNKS // 2:
+                fill_times(nc.vector.tensor_copy, slot + CHUNKS // 2)
+            if work and slot % (QUAD * PERIODS_PER_N) == QUAD * PERIODS_PER_N - 1:
+                invert_denominators(slot // (QUAD * PERIODS_PER_N))
+            for period in due_in(slot - 3):
+                if (period + 1) % (QUAD * PERIODS_PER_N) == 0:
+                    divide_and_store(period // (QUAD * PERIODS_PER_N))

@@ -25,27 +25,25 @@ MOST_NEGATIVE = -80.0
 
 P = 128
 PACK = 4
+PAIR = 2
 PASS_TIMES = P * PACK
-WINDOWS = P // PACK
-GROUPS = M // WINDOWS
-COLS = L // PACK
+PASS_WORDS = PASS_TIMES // PAIR
+PASSES_PER_N = L // PASS_TIMES
 BANK_PASSES = 2
-BANK_COLS = BANK_PASSES * M * PACK
-BANKS = 2
-PERIOD_PASSES = BANKS * BANK_PASSES
-PERIOD_COLS = PERIOD_PASSES * P
-PERIODS_PER_N = COLS // PERIOD_COLS
-PERIODS = N * PERIODS_PER_N
-BLOCK_PERIODS = 4
-FIRST_BLOCKS = (1, 1, 2, 4)
-LAST_BLOCKS = (4, 2, 1, 1)
-BLOCK_COLS = BLOCK_PERIODS * PERIOD_COLS
-BLOCKS_PER_N = 4
+UNIT_PASSES = 4
+X_PASSES = 4
+X_PIECES_PER_N = PASSES_PER_N // X_PASSES
+X_PIECES = N * X_PIECES_PER_N
+X_LEAD = 1
+X_LOADS = 6
+STEPS = (8, 8, 8, 8)
+FIRST_STEPS = (2, 2, 4, 8, 8, 8)
+LAST_STEPS = (8, 8, 8, 4, 2, 1, 1)
+MOST_STEPS = 7
+STEP_TIMES = 8 * PASS_TIMES
+TIME_LOADS = (2, 2, 4, 8, 8, 8)
 QUAD = 4
 SCALAR_BOTH = 4
-X_LOADS = 6
-CHUNK_COLS = PERIOD_COLS
-CHUNKS = COLS // CHUNK_COLS
 
 
 def tile_weightedaggregation_k_kernel(tc, x_aug, t, t_left, t_right, kappa, out):
@@ -53,64 +51,45 @@ def tile_weightedaggregation_k_kernel(tc, x_aug, t, t_left, t_right, kappa, out)
     with ExitStack() as ctx:
         ctx.enter_context(tc.manual_schedule())
         const = ctx.enter_context(tc.tile_pool(name="const", bufs=1))
-        shift_pool = ctx.enter_context(tc.tile_pool(name="shift", bufs=4))
-        sig_pool = ctx.enter_context(tc.tile_pool(name="sig", bufs=4))
-        at_pool = ctx.enter_context(tc.tile_pool(name="alpha_t", bufs=2))
+        sig_pool = ctx.enter_context(tc.tile_pool(name="sig", bufs=2))
+        alpha_pool = ctx.enter_context(tc.tile_pool(name="alpha", bufs=3))
         ag_pool = ctx.enter_context(tc.tile_pool(name="alpha_grouped", bufs=4))
-        aq_pool = ctx.enter_context(tc.tile_pool(name="alpha_q", bufs=3))
+        aq_pool = ctx.enter_context(tc.tile_pool(name="alpha_q", bufs=4))
         xr_pool = ctx.enter_context(tc.tile_pool(name="x_raw", bufs=X_LOADS))
         xg_pool = ctx.enter_context(tc.tile_pool(name="x_grouped", bufs=2))
-        xq_pool = ctx.enter_context(tc.tile_pool(name="x_q", bufs=13))
-        bank_pool = ctx.enter_context(tc.psum_pool(name="banks", bufs=5))
+        xq_pool = ctx.enter_context(tc.tile_pool(name="x_q", bufs=9))
+        bank_pool = ctx.enter_context(tc.psum_pool(name="banks", bufs=6))
         sum_pool = ctx.enter_context(tc.psum_pool(name="sums", bufs=1))
-
-        t_flat = t.rearrange("l o -> (l o)")
-        shift_run = PACK * (CHUNK_COLS - 1) + 1
-        shifted = {}
-
-        def load_shifted(r):
-            run = shift_pool.tile([P, PACK * CHUNK_COLS], BF16)
-            for j in range(PACK):
-                start = PACK * CHUNK_COLS * r + j
-                nc.sync.dma_start(
-                    out=run[j:P:PACK, 0:shift_run],
-                    in_=t_flat[start : start + shift_run].partition_broadcast(WINDOWS),
-                )
-            shifted[r] = run
 
         x_raw = {}
 
-        def load_x(period):
-            if period >= PERIODS:
+        def load_x(piece):
+            if piece >= X_PIECES:
                 return
-            n, part = divmod(period, PERIODS_PER_N)
-            span = PERIOD_PASSES * PASS_TIMES
+            n, part = divmod(piece, X_PIECES_PER_N)
+            span = X_PASSES * PASS_TIMES
             rows = slice(part * span, (part + 1) * span)
-            raw = xr_pool.tile([P, PERIOD_PASSES, B, PACK * F], BF16)
+            raw = xr_pool.tile([P, X_PASSES, B, PACK * F], BF16)
             for b in range(B):
                 nc.sync.dma_start(
                     out=raw[:, :, b],
                     in_=x_aug[b, n, rows, :].rearrange("(c p j) f -> p c (j f)", p=P, j=PACK),
                 )
-            x_raw[period] = raw
+            x_raw[piece] = raw
 
         kappa_b = const.tile([P, N], BF16)
         nc.scalar.dma_start(out=kappa_b[:], in_=kappa.rearrange("n o -> (n o)").partition_broadcast(P))
-        edge_rows = N * GROUPS
-        edges_b = const.tile([2 * edge_rows, WINDOWS], BF16)
-        load_shifted(0)
-        nc.sync.dma_start(
-            out=edges_b[0:edge_rows, :], in_=t_right.rearrange("n (g w) -> (n g) w", w=WINDOWS)
-        )
-        nc.sync.dma_start(
-            out=edges_b[edge_rows : 2 * edge_rows, :],
-            in_=t_left.rearrange("n (g w) -> (n g) w", w=WINDOWS),
-        )
-        load_shifted(1)
-        load_x(0)
-        load_shifted(2)
-        load_shifted(3)
-        load_x(1)
+        edges_b = const.tile([2 * N, M], BF16)
+        nc.scalar.dma_start(out=edges_b[0:N, :], in_=t_right)
+        nc.scalar.dma_start(out=edges_b[N : 2 * N, :], in_=t_left)
+        times = const.tile([P, L], BF16)
+        t_flat = t.rearrange("l o -> (l o)")
+        first = 0
+        for index in range(len(TIME_LOADS)):
+            end = first + TIME_LOADS[index] * PASS_TIMES
+            nc.sync.dma_start(out=times[:, first:end], in_=t_flat[first:end].partition_broadcast(P))
+            first = end
+            load_x(index)
 
         warm = const.tile([P, 1], F32)
         nc.vector.memset(warm[:], 0.0)
@@ -196,219 +175,162 @@ def tile_weightedaggregation_k_kernel(tc, x_aug, t, t_left, t_right, kappa, out)
         neg_inv_k = small("neg_inv_k")
         nc.vector.tensor_scalar_mul(out=neg_inv_k[:], in0=inv_k[:], scalar1=-1.0)
 
-        edges_wide = const.tile([P, P], F32)
-        nc.vector.memset(edges_wide[:], 0.0)
-        nc.vector.tensor_copy(
-            out=edges_wide[0 : 2 * edge_rows, :].rearrange("r (w j) -> r w j", j=PACK),
-            in_=edges_b[:].unsqueeze(2).to_broadcast([2 * edge_rows, WINDOWS, PACK]),
-        )
-        edges_t = sum_pool.tile([P, P], F32, tag="small")
-        nc.tensor.transpose(out=edges_t[:], in_=edges_wide[:], identity=ident_f[:])
-
-        bias_right = const.tile([P, N, GROUPS], F32)
-        nc.vector.tensor_tensor(
-            out=bias_right[:],
-            in0=edges_t[:, 0:edge_rows].rearrange("q (n g) -> q n g", g=GROUPS),
-            in1=inv_k[:].unsqueeze(2).to_broadcast([P, N, GROUPS]),
-            op=ALU.mult,
-        )
-        bias_left = const.tile([P, N, GROUPS], F32)
-        nc.vector.tensor_tensor(
-            out=bias_left[:],
-            in0=edges_t[:, edge_rows : 2 * edge_rows].rearrange("q (n g) -> q n g", g=GROUPS),
-            in1=neg_inv_k[:].unsqueeze(2).to_broadcast([P, N, GROUPS]),
-            op=ALU.mult,
-        )
-
-        times = const.tile([P, COLS], BF16)
-
-        def fill_times(copy, r):
-            copy(
-                out=times[:, r * CHUNK_COLS : (r + 1) * CHUNK_COLS],
-                in_=shifted[r][:].rearrange("q (i j) -> q i j", j=PACK)[:, :, 0],
-            )
-
-        for r in range(CHUNKS // 2):
-            fill_times(nc.scalar.copy, r)
-            load_shifted(r + CHUNKS // 2)
-            load_x(r + 2)
-
-        ident_b = const.tile([P, P], BF16)
-        nc.vector.tensor_copy(out=ident_b[:], in_=ident_f[:])
-        same_window = const.tile([P, WINDOWS], F32)
-        nc.vector.tensor_reduce(
-            out=same_window[:], in_=ident_f[:].rearrange("q (w j) -> q w j", j=PACK),
-            axis=AXIS_X, op=ALU.add,
-        )
-        gather = const.tile([P, GROUPS, M], F32)
-        nc.vector.memset(gather[:], 0.0)
-        for g in range(GROUPS):
-            nc.vector.tensor_copy(
-                out=gather[:, g, g * WINDOWS : (g + 1) * WINDOWS], in_=same_window[:]
-            )
+        edges_rows = const.tile([P, M], F32)
+        nc.vector.memset(edges_rows[:], 0.0)
+        nc.vector.tensor_copy(out=edges_rows[0 : 2 * N, :], in_=edges_b[:])
+        edges_t = bank_pool.tile([P, P], F32, tag="bank")
+        nc.tensor.transpose(out=edges_t[:], in_=edges_rows[:], identity=ident_f[:])
+        bias_right = const.tile([P, N], F32)
+        nc.vector.tensor_mul(out=bias_right[:], in0=edges_t[:, 0:N], in1=inv_k[:])
+        bias_left = const.tile([P, N], F32)
+        nc.vector.tensor_mul(out=bias_left[:], in0=edges_t[:, N : 2 * N], in1=neg_inv_k[:])
 
         x_grouped = {}
         x_q = {}
 
-        def regroup_x(period):
-            if period >= PERIODS:
-                return
-            grouped = xg_pool.tile([P, PERIOD_PASSES, B, F, PACK], BF16, align_bytes=64)
+        def regroup_x(piece):
+            grouped = xg_pool.tile([P, X_PASSES, B, F, PACK], BF16, align_bytes=64)
             nc.vector.tensor_copy(
                 out=grouped[:].rearrange("p c b (r i) j -> p (c b) r j i", i=4),
-                in_=x_raw[period][:].rearrange("p c b (j r i) -> p (c b) r j i", j=PACK, i=4),
+                in_=x_raw[piece][:].rearrange("p c b (j r i) -> p (c b) r j i", j=PACK, i=4),
             )
-            x_grouped[period] = grouped
-            load_x(period + X_LOADS)
+            x_grouped[piece] = grouped
+            load_x(piece + X_LOADS)
 
         def quantise(pool, grouped_flat, words):
-            codes = pool.tile([P, words], U32, align_bytes=64)
-            scales = pool.tile([P, words], U8, align_bytes=64)
-            nc.vector.quantize_mx(out=codes[:].bitcast(FP8X4), scales=scales[:], in_=grouped_flat)
+            codes = pool.tile([P, UNIT_PASSES * P], U32, align_bytes=64)
+            scales = pool.tile([P, UNIT_PASSES * P], U8, align_bytes=64)
+            nc.vector.quantize_mx(
+                out=codes[:, 0:words].bitcast(FP8X4), scales=scales[:, 0:words], in_=grouped_flat
+            )
             return codes, scales
 
-        def quantise_x(period):
-            if period < PERIODS:
-                flat = x_grouped[period][:].rearrange("p c b f j -> p (c b f j)")
-                x_q[period] = quantise(xq_pool, flat, PERIOD_PASSES * P)
+        def quantise_x(piece):
+            flat = x_grouped[piece][:].rearrange("p c b f j -> p (c b f j)")
+            x_q[piece] = quantise(xq_pool, flat, X_PASSES * P)
 
-        blocks = []
+        steps = []
+        units = []
         for n in range(N):
-            widths = (BLOCK_PERIODS,) * (PERIODS_PER_N // BLOCK_PERIODS)
+            widths = STEPS
             if n == 0:
-                widths = FIRST_BLOCKS
+                widths = FIRST_STEPS
             if n == N - 1:
-                widths = LAST_BLOCKS
-            first = n * PERIODS_PER_N
+                widths = LAST_STEPS
+            first = 0
             for place in range(len(widths)):
-                blocks.append((n, place, first, widths[place]))
+                steps.append((n, place, first, widths[place]))
+                unit = min(widths[place], UNIT_PASSES)
+                units.append([(start, unit) for start in range(0, widths[place], unit)])
                 first += widths[place]
-        block_of = {}
-        slots = []
-        due = []
-        ready = []
-        for block in range(len(blocks)):
-            width = blocks[block][3]
-            for s in range(width):
-                share = GROUPS // width
-                slots.append([(block, g) for g in range(s * share, (s + 1) * share)])
-                last = len(slots) > PERIODS - LAST_BLOCKS[0]
-                due.append([ready.pop(0) for taken in range(min(len(ready), 2 if last else 1))])
-            for period in range(blocks[block][2], blocks[block][2] + width):
-                block_of[period] = block
-                ready.append(period)
-        while ready:
-            due.append([ready.pop(0)])
 
-        def due_in(slot):
-            return due[slot] if 0 <= slot < len(due) else []
+        def units_of(step):
+            return [(step, start, size) for start, size in units[step]] if 0 <= step < len(steps) else []
 
         sigmoids = {}
-        alpha_t = {}
-        partial = const.tile([P, N, GROUPS, BLOCKS_PER_N], F32)
+
+        def sigmoid(step, bias, scale, name):
+            n, place, first, width = steps[step]
+            cols = width * PASS_TIMES
+            tile = sig_pool.tile([P, STEP_TIMES], F32, name=name)
+            nc.scalar.activation(
+                out=tile[:, 0:cols], in_=times[:, first * PASS_TIMES : first * PASS_TIMES + cols],
+                func=FUNC.Sigmoid, bias=bias[:, n : n + 1], scale=scale[:, n : n + 1],
+            )
+            sigmoids[(step, name)] = tile
+
+        alpha = {}
+        partial = const.tile([P, N, MOST_STEPS], F32)
         nc.vector.memset(partial[:], 0.0)
 
-        def sigmoid_pair(block, g):
-            n, place, first, width = blocks[block]
-            start = (first - n * PERIODS_PER_N) * PERIOD_COLS
-            cols = width * PERIOD_COLS
-            fall = sig_pool.tile([P, BLOCK_COLS], F32)
-            nc.scalar.activation(
-                out=fall[:, 0:cols], in_=times[:, start : start + cols], func=FUNC.Sigmoid,
-                bias=bias_right[:, n, g : g + 1], scale=neg_inv_k[:, n : n + 1],
-            )
-            rise = sig_pool.tile([P, BLOCK_COLS], F32)
-            nc.scalar.activation(
-                out=rise[:, 0:cols], in_=times[:, start : start + cols], func=FUNC.Sigmoid,
-                bias=bias_left[:, n, g : g + 1], scale=inv_k[:, n : n + 1],
-            )
-            sigmoids[(block, g)] = (fall, rise)
-
-        def product(block, g):
-            n, place, first, width = blocks[block]
-            cols = width * PERIOD_COLS
-            if g == 0:
-                windows_by_time = at_pool.tile([P, GROUPS, BLOCK_COLS], BF16)
-                alpha_t[block] = windows_by_time
-            fall, rise = sigmoids[(block, g)]
+        def product(step):
+            n, place, first, width = steps[step]
+            cols = width * PASS_TIMES
+            rounded = alpha_pool.tile([P, STEP_TIMES], BF16, align_bytes=64)
             nc.vector.scalar_tensor_tensor(
-                out=alpha_t[block][:, g, 0:cols], in0=fall[:, 0:cols], scalar=1.0,
-                in1=rise[:, 0:cols], op0=ALU.mult, op1=ALU.mult,
-                accum_out=partial[:, n, g, place : place + 1],
+                out=rounded[:, 0:cols], in0=sigmoids[(step, "fall")][:, 0:cols], scalar=1.0,
+                in1=sigmoids[(step, "rise")][:, 0:cols], op0=ALU.mult, op1=ALU.mult,
+                accum_out=partial[:, n, place : place + 1],
             )
+            alpha[step] = rounded
 
         banks = {}
 
-        def transpose(period):
-            block = block_of[period]
-            first = (period - blocks[block][2]) * PERIOD_COLS
-            for side in range(BANKS):
-                bank = bank_pool.tile([P, BANK_PASSES, M * PACK], BF16)
-                for c in range(BANK_PASSES):
-                    col = first + (side * BANK_PASSES + c) * P
-                    for g in range(GROUPS):
+        def transpose(unit):
+            step, start, size = unit
+            words = alpha[step][:].bitcast(F32)
+            for side in range(0, size, BANK_PASSES):
+                bank = bank_pool.tile([P, BANK_PASSES, PAIR, M], F32, tag="bank")
+                for c in range(min(size, BANK_PASSES)):
+                    word = (start + side + c) * PASS_WORDS
+                    for u in range(PAIR):
                         nc.tensor.transpose(
-                            out=bank[:, c, g * P : (g + 1) * P],
-                            in_=alpha_t[block][:, g, col : col + P],
-                            identity=ident_b[:],
+                            out=bank[:, c, u, :],
+                            in_=words[:, word + u : word + PASS_WORDS : PAIR],
+                            identity=ident_f[:],
                         )
-                banks[(period, side)] = bank
+                banks[(unit, side)] = bank
 
         alpha_grouped = {}
         alpha_q = {}
+        emptied = []
 
-        def empty_banks(period):
-            grouped = ag_pool.tile([P, BANKS * BANK_COLS], BF16, align_bytes=64)
-            for side in range(BANKS):
-                dst = grouped[:, side * BANK_COLS : (side + 1) * BANK_COLS]
-                src = banks[(period, side)][:].rearrange("p c w -> p (c w)")
-                if side == 0 or period % SCALAR_BOTH == 0:
+        def empty_banks(unit):
+            step, start, size = unit
+            grouped = ag_pool.tile([P, UNIT_PASSES * M * PACK], BF16, align_bytes=64)
+            words = grouped[:].bitcast(F32).rearrange("p (c m u) -> p c m u", m=M, u=PAIR)
+            for side in range(0, size, BANK_PASSES):
+                end = side + min(size, BANK_PASSES)
+                dst = words[:, side:end]
+                src = banks[(unit, side)][:, 0 : end - side].rearrange("p c u m -> p c m u")
+                if side == 0 or len(emptied) % SCALAR_BOTH == 0:
                     nc.scalar.copy(out=dst, in_=src)
                 else:
                     nc.vector.tensor_copy(out=dst, in_=src)
-            alpha_grouped[period] = grouped
+            emptied.append(unit)
+            alpha_grouped[unit] = grouped
 
-        def quantise_alpha(period):
-            alpha_q[period] = quantise(aq_pool, alpha_grouped[period][:], PERIOD_PASSES * P)
+        def quantise_alpha(unit):
+            step, start, size = unit
+            flat = alpha_grouped[unit][:, 0 : size * M * PACK]
+            alpha_q[unit] = quantise(aq_pool, flat, size * M)
 
         numerators = {}
 
-        def multiply(period):
-            n, part = divmod(period, PERIODS_PER_N)
-            quad, place = divmod(n, QUAD)
-            if place == 0 and part == 0:
+        def multiply(unit):
+            step, start, size = unit
+            n, place, first, width = steps[step]
+            quad, channel = divmod(n, QUAD)
+            if channel == 0 and first + start == 0:
                 numerator = sum_pool.tile([P, QUAD, B * F], F32, name="numerator%d" % quad)
                 numerators[quad] = numerator
-            a_codes, a_scales = alpha_q[period]
-            x_codes, x_scales = x_q[period]
-            for c in range(PERIOD_PASSES):
-                words = slice(c * P, (c + 1) * P)
+            a_codes, a_scales = alpha_q[unit]
+            for c in range(size):
+                passed = first + start + c
+                piece, part = divmod(n * PASSES_PER_N + passed, X_PASSES)
+                x_codes, x_scales = x_q[piece]
+                a_words = slice(c * P, (c + 1) * P)
+                x_words = slice(part * P, (part + 1) * P)
                 nc.tensor.matmul_mx(
-                    out=numerators[quad][:, place, :],
-                    lhsT=a_codes[:, words].bitcast(FP8X4),
-                    lhsT_scale=a_scales[:, words],
-                    rhs=x_codes[:, words].bitcast(FP8X4),
-                    rhs_scale=x_scales[:, words],
-                    start=(part == 0 and c == 0),
-                    stop=(part == PERIODS_PER_N - 1 and c == PERIOD_PASSES - 1),
+                    out=numerators[quad][:, channel, :],
+                    lhsT=a_codes[:, a_words].bitcast(FP8X4),
+                    lhsT_scale=a_scales[:, a_words],
+                    rhs=x_codes[:, x_words].bitcast(FP8X4),
+                    rhs_scale=x_scales[:, x_words],
+                    start=(passed == 0),
+                    stop=(passed == PASSES_PER_N - 1),
                 )
 
         inv_den = const.tile([P, N], F32)
 
         def invert_denominators(quad):
             channels = slice(QUAD * quad, QUAD * (quad + 1))
-            by_group = const.tile([P, GROUPS, QUAD], F32, name="by_group%d" % quad)
             nc.vector.tensor_reduce(
-                out=by_group[:], in_=partial[:, channels].rearrange("q n g h -> q g n h"),
-                axis=AXIS_X, op=ALU.add,
+                out=inv_den[:, channels], in_=partial[:, channels], axis=AXIS_X, op=ALU.add
             )
-            denominator = sum_pool.tile([P, QUAD], F32, tag="small")
-            for g in range(GROUPS):
-                nc.tensor.matmul(
-                    out=denominator[:], lhsT=gather[:, g, :], rhs=by_group[:, g, :],
-                    start=(g == 0), stop=(g == GROUPS - 1),
-                )
-            nc.vector.tensor_scalar_add(out=inv_den[:, channels], in0=denominator[:], scalar1=EPS)
+            nc.vector.tensor_scalar_add(
+                out=inv_den[:, channels], in0=inv_den[:, channels], scalar1=EPS
+            )
             nc.vector.reciprocal(out=inv_den[:, channels], in_=inv_den[:, channels])
 
         def divide_and_store(quad):
@@ -427,31 +349,40 @@ def tile_weightedaggregation_k_kernel(tc, x_aug, t, t_left, t_right, kappa, out)
 
         x_regrouped = 0
         x_quantised = 0
-        for slot in range(len(due) + 3):
-            work = slots[slot] if slot < len(slots) else []
-            for block, g in work:
-                sigmoid_pair(block, g)
-            for period in due_in(slot - 3):
-                multiply(period)
-            for period in due_in(slot - 1):
-                empty_banks(period)
-            for period in due_in(slot):
-                transpose(period)
-            for period in due_in(slot - 2):
-                quantise_alpha(period)
-            for turn in range(1 if due_in(slot - 1) else 2):
+        for turn in range(len(steps) + 2):
+            if turn < len(steps):
+                sigmoid(turn, bias_right, neg_inv_k, "fall")
+            for unit in units_of(turn - 2):
+                empty_banks(unit)
+            if turn < len(steps):
+                sigmoid(turn, bias_left, inv_k, "rise")
+            for unit in units_of(turn - 1):
+                transpose(unit)
+            wanted = X_PIECES
+            if turn == 0:
+                wanted = 0
+            elif turn < len(steps):
+                n, place, first, width = steps[turn]
+                passes = n * PASSES_PER_N + first + width
+                wanted = min(X_PIECES, (passes + X_PASSES - 1) // X_PASSES + X_LEAD)
+            pending = units_of(turn - 2)
+            while pending or x_quantised < wanted:
                 if x_quantised < x_regrouped:
                     quantise_x(x_quantised)
                     x_quantised += 1
-                if x_regrouped < PERIODS:
+                if x_regrouped < X_PIECES and x_regrouped < wanted + 1:
                     regroup_x(x_regrouped)
                     x_regrouped += 1
-            for block, g in work:
-                product(block, g)
-            if slot < CHUNKS // 2:
-                fill_times(nc.vector.tensor_copy, slot + CHUNKS // 2)
-            if work and slot % (QUAD * PERIODS_PER_N) == QUAD * PERIODS_PER_N - 1:
-                invert_denominators(slot // (QUAD * PERIODS_PER_N))
-            for period in due_in(slot - 3):
-                if (period + 1) % (QUAD * PERIODS_PER_N) == 0:
-                    divide_and_store(period // (QUAD * PERIODS_PER_N))
+                if pending:
+                    quantise_alpha(pending.pop(0))
+            for unit in units_of(turn - 2):
+                multiply(unit)
+            if turn < len(steps):
+                product(turn)
+                n, place, first, width = steps[turn]
+                if first + width == PASSES_PER_N and (n + 1) % QUAD == 0:
+                    invert_denominators(n // QUAD)
+            if 2 <= turn:
+                n, place, first, width = steps[turn - 2]
+                if first + width == PASSES_PER_N and (n + 1) % QUAD == 0:
+                    divide_and_store(n // QUAD)

@@ -18,8 +18,6 @@ EPS = 1e-8
 FLOPS = 2 * B * N * M * F * L
 
 LN2 = 0.6931471805599453
-LN2_HIGH = 0.693145751953125
-LN2_LOW = LN2 - LN2_HIGH
 LOG2_E = 1.4426950408889634
 MOST_NEGATIVE = -80.0
 
@@ -30,12 +28,11 @@ PASS_TIMES = P * PACK
 PASS_WORDS = PASS_TIMES // PAIR
 PASSES_PER_N = L // PASS_TIMES
 BANK_PASSES = 2
-UNIT_PASSES = 4
-X_PASSES = 4
+UNIT_PASSES = 8
+X_PASSES = 8
 X_PIECES_PER_N = PASSES_PER_N // X_PASSES
 X_PIECES = N * X_PIECES_PER_N
-X_LEAD = 1
-X_LOADS = 6
+X_LOADS = 4
 STEPS = (8, 8, 8, 8)
 FIRST_STEPS = (2, 2, 4, 8, 8, 8)
 LAST_STEPS = (8, 8, 8, 4, 2, 1, 1)
@@ -43,7 +40,8 @@ MOST_STEPS = 7
 STEP_TIMES = 8 * PASS_TIMES
 TIME_LOADS = (2, 2, 4, 8, 8, 8)
 QUAD = 4
-SCALAR_BOTH = 4
+HEAD_ROWS = 8
+SCALAR_BANKS = (3, 2, 2)
 
 
 def tile_weightedaggregation_k_kernel(tc, x_aug, t, t_left, t_right, kappa, out):
@@ -51,13 +49,14 @@ def tile_weightedaggregation_k_kernel(tc, x_aug, t, t_left, t_right, kappa, out)
     with ExitStack() as ctx:
         ctx.enter_context(tc.manual_schedule())
         const = ctx.enter_context(tc.tile_pool(name="const", bufs=1))
-        sig_pool = ctx.enter_context(tc.tile_pool(name="sig", bufs=2))
-        alpha_pool = ctx.enter_context(tc.tile_pool(name="alpha", bufs=3))
-        ag_pool = ctx.enter_context(tc.tile_pool(name="alpha_grouped", bufs=4))
-        aq_pool = ctx.enter_context(tc.tile_pool(name="alpha_q", bufs=4))
+        fall_pool = ctx.enter_context(tc.tile_pool(name="fall", bufs=2))
+        rise_pool = ctx.enter_context(tc.tile_pool(name="rise", bufs=2))
+        alpha_pool = ctx.enter_context(tc.tile_pool(name="alpha", bufs=2))
+        ag_pool = ctx.enter_context(tc.tile_pool(name="alpha_grouped", bufs=2))
+        aq_pool = ctx.enter_context(tc.tile_pool(name="alpha_q", bufs=3))
         xr_pool = ctx.enter_context(tc.tile_pool(name="x_raw", bufs=X_LOADS))
         xg_pool = ctx.enter_context(tc.tile_pool(name="x_grouped", bufs=2))
-        xq_pool = ctx.enter_context(tc.tile_pool(name="x_q", bufs=9))
+        xq_pool = ctx.enter_context(tc.tile_pool(name="x_q", bufs=5))
         bank_pool = ctx.enter_context(tc.psum_pool(name="banks", bufs=6))
         sum_pool = ctx.enter_context(tc.psum_pool(name="sums", bufs=1))
 
@@ -89,7 +88,8 @@ def tile_weightedaggregation_k_kernel(tc, x_aug, t, t_left, t_right, kappa, out)
             end = first + TIME_LOADS[index] * PASS_TIMES
             nc.sync.dma_start(out=times[:, first:end], in_=t_flat[first:end].partition_broadcast(P))
             first = end
-            load_x(index)
+            if index < X_LOADS:
+                load_x(index)
 
         warm = const.tile([P, 1], F32)
         nc.vector.memset(warm[:], 0.0)
@@ -106,28 +106,28 @@ def tile_weightedaggregation_k_kernel(tc, x_aug, t, t_left, t_right, kappa, out)
                 out=out[:], in0=in0[:], scalar=scalar, in1=in1[:], op0=ALU.add, op1=ALU.mult
             )
 
+        edges_rows = const.tile([P, M], F32)
+        nc.vector.memset(edges_rows[:], 0.0)
         minus_abs = small("minus_abs")
         nc.vector.scalar_tensor_tensor(
             out=minus_abs[:], in0=kappa_b[:], scalar=-1.0, in1=kappa_b[:], op0=ALU.mult, op1=ALU.min
         )
         kappa_relu = small("kappa_relu")
         nc.vector.tensor_scalar_max(out=kappa_relu[:], in0=kappa_b[:], scalar1=0.0)
-        nc.vector.tensor_scalar_max(out=minus_abs[:], in0=minus_abs[:], scalar1=MOST_NEGATIVE)
         power_i = small("power_i", I32)
-        nc.vector.tensor_scalar_mul(out=power_i[:], in0=minus_abs[:], scalar1=LOG2_E)
-        power = small("power")
-        nc.vector.tensor_copy(out=power[:], in_=power_i[:])
+        nc.vector.tensor_scalar(
+            out=power_i[:], in0=minus_abs[:], scalar1=LOG2_E, scalar2=MOST_NEGATIVE * LOG2_E,
+            op0=ALU.mult, op1=ALU.max,
+        )
+        nc.vector.tensor_scalar_max(out=minus_abs[:], in0=minus_abs[:], scalar1=MOST_NEGATIVE)
         r = small("r")
         nc.vector.scalar_tensor_tensor(
-            out=r[:], in0=power[:], scalar=-LN2_HIGH, in1=minus_abs[:], op0=ALU.mult, op1=ALU.add
+            out=r[:], in0=power_i[:], scalar=-LN2, in1=minus_abs[:], op0=ALU.mult, op1=ALU.add
         )
         two_to_power = small("two_to_power", I32)
         nc.vector.tensor_scalar(
-            out=two_to_power[:], in0=power[:], scalar1=127.0, scalar2=8388608.0,
+            out=two_to_power[:], in0=power_i[:], scalar1=127.0, scalar2=8388608.0,
             op0=ALU.add, op1=ALU.mult,
-        )
-        nc.vector.scalar_tensor_tensor(
-            out=r[:], in0=power[:], scalar=-LN2_LOW, in1=r[:], op0=ALU.mult, op1=ALU.add
         )
         r2 = small("r2")
         nc.vector.tensor_mul(out=r2[:], in0=r[:], in1=r[:])
@@ -147,6 +147,9 @@ def tile_weightedaggregation_k_kernel(tc, x_aug, t, t_left, t_right, kappa, out)
             out=e_den[:], in0=even[:], scalar=1008.0, in1=odd[:], op0=ALU.add, op1=ALU.subtract
         )
         nc.vector.tensor_mul(out=e_num[:], in0=e_num[:], in1=two_to_power[:].bitcast(F32))
+        nc.vector.tensor_copy(out=edges_rows[0 : 2 * N, :], in_=edges_b[:])
+        edges_t = bank_pool.tile([P, P], F32, tag="bank")
+        nc.tensor.transpose(out=edges_t[:], in_=edges_rows[:], identity=ident_f[:])
         z = small("z")
         nc.vector.scalar_tensor_tensor(
             out=z[:], in0=e_den[:], scalar=2.0, in1=e_num[:], op0=ALU.mult, op1=ALU.add
@@ -155,47 +158,51 @@ def tile_weightedaggregation_k_kernel(tc, x_aug, t, t_left, t_right, kappa, out)
         nc.vector.tensor_mul(out=z[:], in0=z[:], in1=e_num[:])
         y = small("y")
         nc.vector.tensor_mul(out=y[:], in0=z[:], in1=z[:])
-        top = small("top")
-        nc.vector.tensor_scalar_mul(out=top[:], in0=y[:], scalar1=-256.0)
         bottom = small("bottom")
-        nc.vector.tensor_scalar_mul(out=bottom[:], in0=y[:], scalar1=-1225.0)
-        add_mult(top, top, 5943.0, y)
-        add_mult(bottom, bottom, 11025.0, y)
-        add_mult(top, top, -19250.0, y)
-        add_mult(bottom, bottom, -24255.0, y)
-        add_mult(top, top, 15015.0, z)
-        nc.vector.tensor_scalar_add(out=bottom[:], in0=bottom[:], scalar1=15015.0)
+        nc.vector.tensor_scalar_mul(out=bottom[:], in0=y[:], scalar1=225.0)
+        top = small("top")
+        nc.vector.tensor_scalar_mul(out=top[:], in0=y[:], scalar1=64.0)
+        add_mult(bottom, bottom, -1050.0, y)
+        add_mult(top, top, -735.0, y)
+        nc.vector.tensor_scalar_add(out=bottom[:], in0=bottom[:], scalar1=945.0)
+        add_mult(top, top, 945.0, z)
+        right_bottom = small("right_bottom")
+        nc.vector.tensor_mul(out=right_bottom[:], in0=edges_t[:, 0:N], in1=bottom[:])
         nc.vector.tensor_mul(out=kappa_relu[:], in0=kappa_relu[:], in1=bottom[:])
         inv_k = small("inv_k")
         nc.vector.scalar_tensor_tensor(
             out=inv_k[:], in0=top[:], scalar=2.0, in1=kappa_relu[:], op0=ALU.mult, op1=ALU.add
         )
         nc.vector.reciprocal(out=inv_k[:], in_=inv_k[:])
-        nc.vector.tensor_mul(out=inv_k[:], in0=inv_k[:], in1=bottom[:])
         neg_inv_k = small("neg_inv_k")
-        nc.vector.tensor_scalar_mul(out=neg_inv_k[:], in0=inv_k[:], scalar1=-1.0)
-
-        edges_rows = const.tile([P, M], F32)
-        nc.vector.memset(edges_rows[:], 0.0)
-        nc.vector.tensor_copy(out=edges_rows[0 : 2 * N, :], in_=edges_b[:])
-        edges_t = bank_pool.tile([P, P], F32, tag="bank")
-        nc.tensor.transpose(out=edges_t[:], in_=edges_rows[:], identity=ident_f[:])
-        bias_right = const.tile([P, N], F32)
-        nc.vector.tensor_mul(out=bias_right[:], in0=edges_t[:, 0:N], in1=inv_k[:])
-        bias_left = const.tile([P, N], F32)
+        nc.vector.scalar_tensor_tensor(
+            out=neg_inv_k[:], in0=inv_k[:], scalar=-1.0, in1=bottom[:], op0=ALU.mult, op1=ALU.mult
+        )
+        bias_right = small("bias_right")
+        nc.vector.tensor_mul(out=bias_right[:], in0=right_bottom[:], in1=inv_k[:])
+        nc.vector.tensor_mul(out=inv_k[:], in0=inv_k[:], in1=bottom[:])
+        bias_left = small("bias_left")
         nc.vector.tensor_mul(out=bias_left[:], in0=edges_t[:, N : 2 * N], in1=neg_inv_k[:])
 
         x_grouped = {}
         x_q = {}
 
         def regroup_x(piece):
-            grouped = xg_pool.tile([P, X_PASSES, B, F, PACK], BF16, align_bytes=64)
-            nc.vector.tensor_copy(
-                out=grouped[:].rearrange("p c b (r i) j -> p (c b) r j i", i=4),
-                in_=x_raw[piece][:].rearrange("p c b (j r i) -> p (c b) r j i", j=PACK, i=4),
-            )
-            x_grouped[piece] = grouped
+            if piece not in x_grouped:
+                grouped = xg_pool.tile([P, X_PASSES, B, F, PACK], BF16, align_bytes=64)
+                x_grouped[piece] = grouped
+            rows = slice(HEAD_ROWS if piece == 0 else 0, X_PASSES * B)
+            copy_rows(nc.vector.tensor_copy, piece, rows)
             load_x(piece + X_LOADS)
+
+        def copy_rows(copy, piece, rows):
+            dst = x_grouped[piece][:].rearrange("p c b (r i) j -> p (c b) r j i", i=4)
+            src = x_raw[piece][:].rearrange("p c b (j r i) -> p (c b) r j i", j=PACK, i=4)
+            copy(out=dst[:, rows], in_=src[:, rows])
+
+        head = xg_pool.tile([P, X_PASSES, B, F, PACK], BF16, align_bytes=64, name="grouped")
+        x_grouped[0] = head
+        copy_rows(nc.scalar.copy, 0, slice(0, HEAD_ROWS))
 
         def quantise(pool, grouped_flat, words):
             codes = pool.tile([P, UNIT_PASSES * P], U32, align_bytes=64)
@@ -229,10 +236,10 @@ def tile_weightedaggregation_k_kernel(tc, x_aug, t, t_left, t_right, kappa, out)
 
         sigmoids = {}
 
-        def sigmoid(step, bias, scale, name):
+        def sigmoid(step, pool, bias, scale, name):
             n, place, first, width = steps[step]
             cols = width * PASS_TIMES
-            tile = sig_pool.tile([P, STEP_TIMES], F32, name=name)
+            tile = pool.tile([P, STEP_TIMES], F32, name=name)
             nc.scalar.activation(
                 out=tile[:, 0:cols], in_=times[:, first * PASS_TIMES : first * PASS_TIMES + cols],
                 func=FUNC.Sigmoid, bias=bias[:, n : n + 1], scale=scale[:, n : n + 1],
@@ -273,7 +280,6 @@ def tile_weightedaggregation_k_kernel(tc, x_aug, t, t_left, t_right, kappa, out)
 
         alpha_grouped = {}
         alpha_q = {}
-        emptied = []
 
         def empty_banks(unit):
             step, start, size = unit
@@ -283,11 +289,10 @@ def tile_weightedaggregation_k_kernel(tc, x_aug, t, t_left, t_right, kappa, out)
                 end = side + min(size, BANK_PASSES)
                 dst = words[:, side:end]
                 src = banks[(unit, side)][:, 0 : end - side].rearrange("p c u m -> p c m u")
-                if side == 0 or len(emptied) % SCALAR_BOTH == 0:
+                if side < BANK_PASSES * SCALAR_BANKS[step % len(SCALAR_BANKS)]:
                     nc.scalar.copy(out=dst, in_=src)
                 else:
                     nc.vector.tensor_copy(out=dst, in_=src)
-            emptied.append(unit)
             alpha_grouped[unit] = grouped
 
         def quantise_alpha(unit):
@@ -351,11 +356,11 @@ def tile_weightedaggregation_k_kernel(tc, x_aug, t, t_left, t_right, kappa, out)
         x_quantised = 0
         for turn in range(len(steps) + 2):
             if turn < len(steps):
-                sigmoid(turn, bias_right, neg_inv_k, "fall")
+                sigmoid(turn, fall_pool, bias_right, neg_inv_k, "fall")
             for unit in units_of(turn - 2):
                 empty_banks(unit)
             if turn < len(steps):
-                sigmoid(turn, bias_left, inv_k, "rise")
+                sigmoid(turn, rise_pool, bias_left, inv_k, "rise")
             for unit in units_of(turn - 1):
                 transpose(unit)
             wanted = X_PIECES
@@ -364,7 +369,7 @@ def tile_weightedaggregation_k_kernel(tc, x_aug, t, t_left, t_right, kappa, out)
             elif turn < len(steps):
                 n, place, first, width = steps[turn]
                 passes = n * PASSES_PER_N + first + width
-                wanted = min(X_PIECES, (passes + X_PASSES - 1) // X_PASSES + X_LEAD)
+                wanted = (passes + X_PASSES - 1) // X_PASSES
             pending = units_of(turn - 2)
             while pending or x_quantised < wanted:
                 if x_quantised < x_regrouped:

@@ -39,8 +39,9 @@ LAST_STEPS = (8, 8, 8, 4, 2, 1, 1)
 MOST_STEPS = 7
 STEP_TIMES = 8 * PASS_TIMES
 TIME_LOADS = (2, 2, 4, 8, 8, 8)
-QUAD = 4
-HEAD_ROWS = 8
+SETS = ((0, 4), (4, 7), (7, 8))
+MOST_SET = 4
+HEAD_ROWS = 14
 SCALAR_BANKS = (3, 2, 2)
 
 
@@ -58,7 +59,7 @@ def tile_weightedaggregation_k_kernel(tc, x_aug, t, t_left, t_right, kappa, out)
         xg_pool = ctx.enter_context(tc.tile_pool(name="x_grouped", bufs=2))
         xq_pool = ctx.enter_context(tc.tile_pool(name="x_q", bufs=5))
         bank_pool = ctx.enter_context(tc.psum_pool(name="banks", bufs=6))
-        sum_pool = ctx.enter_context(tc.psum_pool(name="sums", bufs=1))
+        sum_pool = ctx.enter_context(tc.psum_pool(name="sums", bufs=2))
 
         x_raw = {}
 
@@ -85,11 +86,11 @@ def tile_weightedaggregation_k_kernel(tc, x_aug, t, t_left, t_right, kappa, out)
         t_flat = t.rearrange("l o -> (l o)")
         first = 0
         for index in range(len(TIME_LOADS)):
+            if index < X_LOADS:
+                load_x(index)
             end = first + TIME_LOADS[index] * PASS_TIMES
             nc.sync.dma_start(out=times[:, first:end], in_=t_flat[first:end].partition_broadcast(P))
             first = end
-            if index < X_LOADS:
-                load_x(index)
 
         warm = const.tile([P, 1], F32)
         nc.vector.memset(warm[:], 0.0)
@@ -302,13 +303,16 @@ def tile_weightedaggregation_k_kernel(tc, x_aug, t, t_left, t_right, kappa, out)
 
         numerators = {}
 
+        def set_of(n):
+            return [channels for channels in SETS if channels[0] <= n < channels[1]][0]
+
         def multiply(unit):
             step, start, size = unit
             n, place, first, width = steps[step]
-            quad, channel = divmod(n, QUAD)
-            if channel == 0 and first + start == 0:
-                numerator = sum_pool.tile([P, QUAD, B * F], F32, name="numerator%d" % quad)
-                numerators[quad] = numerator
+            begin, end = set_of(n)
+            if n == begin and first + start == 0:
+                numerator = sum_pool.tile([P, MOST_SET, B * F], F32, tag="numerator")
+                numerators[begin] = numerator
             a_codes, a_scales = alpha_q[unit]
             for c in range(size):
                 passed = first + start + c
@@ -317,7 +321,7 @@ def tile_weightedaggregation_k_kernel(tc, x_aug, t, t_left, t_right, kappa, out)
                 a_words = slice(c * P, (c + 1) * P)
                 x_words = slice(part * P, (part + 1) * P)
                 nc.tensor.matmul_mx(
-                    out=numerators[quad][:, channel, :],
+                    out=numerators[begin][:, n - begin, :],
                     lhsT=a_codes[:, a_words].bitcast(FP8X4),
                     lhsT_scale=a_scales[:, a_words],
                     rhs=x_codes[:, x_words].bitcast(FP8X4),
@@ -328,28 +332,27 @@ def tile_weightedaggregation_k_kernel(tc, x_aug, t, t_left, t_right, kappa, out)
 
         inv_den = const.tile([P, N], F32)
 
-        def invert_denominators(quad):
-            channels = slice(QUAD * quad, QUAD * (quad + 1))
+        def invert_denominators(begin, end):
             nc.vector.tensor_reduce(
-                out=inv_den[:, channels], in_=partial[:, channels], axis=AXIS_X, op=ALU.add
+                out=inv_den[:, begin:end], in_=partial[:, begin:end], axis=AXIS_X, op=ALU.add
             )
             nc.vector.tensor_scalar_add(
-                out=inv_den[:, channels], in0=inv_den[:, channels], scalar1=EPS
+                out=inv_den[:, begin:end], in0=inv_den[:, begin:end], scalar1=EPS
             )
-            nc.vector.reciprocal(out=inv_den[:, channels], in_=inv_den[:, channels])
+            nc.vector.reciprocal(out=inv_den[:, begin:end], in_=inv_den[:, begin:end])
 
-        def divide_and_store(quad):
-            channels = slice(QUAD * quad, QUAD * (quad + 1))
-            result = const.tile([P, QUAD, B, F], F32, name="result%d" % quad)
+        def divide_and_store(begin, end):
+            count = end - begin
+            result = const.tile([P, count, B, F], F32, name="result%d" % begin)
             nc.vector.tensor_tensor(
                 out=result[:].rearrange("m n b f -> m n (b f)"),
-                in0=numerators[quad][:],
-                in1=inv_den[:, channels].unsqueeze(2).to_broadcast([P, QUAD, B * F]),
+                in0=numerators[begin][:, 0:count],
+                in1=inv_den[:, begin:end].unsqueeze(2).to_broadcast([P, count, B * F]),
                 op=ALU.mult,
             )
             for b in range(B):
                 nc.sync.dma_start(
-                    out=out[b, channels].rearrange("n m f -> m n f"), in_=result[:, :, b, :]
+                    out=out[b, begin:end].rearrange("n m f -> m n f"), in_=result[:, :, b, :]
                 )
 
         x_regrouped = 0
@@ -375,19 +378,21 @@ def tile_weightedaggregation_k_kernel(tc, x_aug, t, t_left, t_right, kappa, out)
                 if x_quantised < x_regrouped:
                     quantise_x(x_quantised)
                     x_quantised += 1
+                if pending:
+                    quantise_alpha(pending.pop(0))
                 if x_regrouped < X_PIECES and x_regrouped < wanted + 1:
                     regroup_x(x_regrouped)
                     x_regrouped += 1
-                if pending:
-                    quantise_alpha(pending.pop(0))
             for unit in units_of(turn - 2):
                 multiply(unit)
             if turn < len(steps):
                 product(turn)
                 n, place, first, width = steps[turn]
-                if first + width == PASSES_PER_N and (n + 1) % QUAD == 0:
-                    invert_denominators(n // QUAD)
+                begin, end = set_of(n)
+                if first + width == PASSES_PER_N and n + 1 == end:
+                    invert_denominators(begin, end)
             if 2 <= turn:
                 n, place, first, width = steps[turn - 2]
-                if first + width == PASSES_PER_N and (n + 1) % QUAD == 0:
-                    divide_and_store(n // QUAD)
+                begin, end = set_of(n)
+                if first + width == PASSES_PER_N and n + 1 == end:
+                    divide_and_store(begin, end)

from contextlib import ExitStack

import concourse.mybir as mybir
from concourse.masks import make_identity

F32 = mybir.dt.float32
BF16 = mybir.dt.bfloat16
I32 = mybir.dt.int32
U32 = mybir.dt.uint32
U8 = mybir.dt.uint8
FP8X4 = mybir.dt.float8_e4m3fn_x4
FUNC = mybir.ActivationFunctionType
ALU = mybir.AluOpType
AXIS_X = mybir.AxisListType.X

B, N, L, M, F = 2, 8, 16384, 128, 64
EPS = 1e-8
FLOPS = 2 * B * N * M * F * L

LN2 = 0.6931471805599453
LOG2_E = 1.4426950408889634
MOST_NEGATIVE = -80.0

P = 128
PACK = 4
PAIR = 2
PASS_TIMES = P * PACK
PASS_WORDS = PASS_TIMES // PAIR
PASSES_PER_N = L // PASS_TIMES
BANK_PASSES = 2
UNIT_PASSES = 8
X_PASSES = 8
X_PIECES_PER_N = PASSES_PER_N // X_PASSES
X_PIECES = N * X_PIECES_PER_N
X_LOADS = 4
STEPS = (8, 8, 8, 8)
FIRST_STEPS = (2, 2, 4, 8, 8, 8)
LAST_STEPS = (8, 8, 8, 4, 2, 1, 1)
MOST_STEPS = 7
STEP_TIMES = 8 * PASS_TIMES
TIME_LOADS = (2, 2, 4, 8, 8, 8)
SETS = ((0, 4), (4, 7), (7, 8))
MOST_SET = 4
HEAD_ROWS = 14
SCALAR_BANKS = (3, 2, 2)


def tile_weightedaggregation_k_kernel(tc, x_aug, t, t_left, t_right, kappa, out):
    nc = tc.nc
    with ExitStack() as ctx:
        ctx.enter_context(tc.manual_schedule())
        const = ctx.enter_context(tc.tile_pool(name="const", bufs=1))
        fall_pool = ctx.enter_context(tc.tile_pool(name="fall", bufs=2))
        rise_pool = ctx.enter_context(tc.tile_pool(name="rise", bufs=2))
        alpha_pool = ctx.enter_context(tc.tile_pool(name="alpha", bufs=2))
        ag_pool = ctx.enter_context(tc.tile_pool(name="alpha_grouped", bufs=2))
        aq_pool = ctx.enter_context(tc.tile_pool(name="alpha_q", bufs=3))
        xr_pool = ctx.enter_context(tc.tile_pool(name="x_raw", bufs=X_LOADS))
        xg_pool = ctx.enter_context(tc.tile_pool(name="x_grouped", bufs=2))
        xq_pool = ctx.enter_context(tc.tile_pool(name="x_q", bufs=5))
        bank_pool = ctx.enter_context(tc.psum_pool(name="banks", bufs=6))
        sum_pool = ctx.enter_context(tc.psum_pool(name="sums", bufs=2))

        x_raw = {}

        def load_x(piece):
            if piece >= X_PIECES:
                return
            n, part = divmod(piece, X_PIECES_PER_N)
            span = X_PASSES * PASS_TIMES
            rows = slice(part * span, (part + 1) * span)
            raw = xr_pool.tile([P, X_PASSES, B, PACK * F], BF16)
            for b in range(B):
                nc.sync.dma_start(
                    out=raw[:, :, b],
                    in_=x_aug[b, n, rows, :].rearrange("(c p j) f -> p c (j f)", p=P, j=PACK),
                )
            x_raw[piece] = raw

        kappa_b = const.tile([P, N], BF16)
        nc.scalar.dma_start(out=kappa_b[:], in_=kappa.rearrange("n o -> (n o)").partition_broadcast(P))
        edges_b = const.tile([2 * N, M], BF16)
        nc.scalar.dma_start(out=edges_b[0:N, :], in_=t_right)
        nc.scalar.dma_start(out=edges_b[N : 2 * N, :], in_=t_left)
        times = const.tile([P, L], BF16)
        t_flat = t.rearrange("l o -> (l o)")
        first = 0
        for index in range(len(TIME_LOADS)):
            if index < X_LOADS:
                load_x(index)
            end = first + TIME_LOADS[index] * PASS_TIMES
            nc.sync.dma_start(out=times[:, first:end], in_=t_flat[first:end].partition_broadcast(P))
            first = end

        warm = const.tile([P, 1], F32)
        nc.vector.memset(warm[:], 0.0)
        nc.scalar.activation(out=warm[:], in_=warm[:], func=FUNC.Sigmoid)

        ident_f = const.tile([P, P], F32)
        make_identity(nc, ident_f[:])

        def small(name, dtype=F32):
            return const.tile([P, N], dtype, name=name)

        def add_mult(out, in0, scalar, in1):
            nc.vector.scalar_tensor_tensor(
                out=out[:], in0=in0[:], scalar=scalar, in1=in1[:], op0=ALU.add, op1=ALU.mult
            )

        edges_rows = const.tile([P, M], F32)
        nc.vector.memset(edges_rows[:], 0.0)
        minus_abs = small("minus_abs")
        nc.vector.scalar_tensor_tensor(
            out=minus_abs[:], in0=kappa_b[:], scalar=-1.0, in1=kappa_b[:], op0=ALU.mult, op1=ALU.min
        )
        kappa_relu = small("kappa_relu")
        nc.vector.tensor_scalar_max(out=kappa_relu[:], in0=kappa_b[:], scalar1=0.0)
        power_i = small("power_i", I32)
        nc.vector.tensor_scalar(
            out=power_i[:], in0=minus_abs[:], scalar1=LOG2_E, scalar2=MOST_NEGATIVE * LOG2_E,
            op0=ALU.mult, op1=ALU.max,
        )
        nc.vector.tensor_scalar_max(out=minus_abs[:], in0=minus_abs[:], scalar1=MOST_NEGATIVE)
        r = small("r")
        nc.vector.scalar_tensor_tensor(
            out=r[:], in0=power_i[:], scalar=-LN2, in1=minus_abs[:], op0=ALU.mult, op1=ALU.add
        )
        two_to_power = small("two_to_power", I32)
        nc.vector.tensor_scalar(
            out=two_to_power[:], in0=power_i[:], scalar1=127.0, scalar2=8388608.0,
            op0=ALU.add, op1=ALU.mult,
        )
        r2 = small("r2")
        nc.vector.tensor_mul(out=r2[:], in0=r[:], in1=r[:])
        r_30th = small("r_30th")
        nc.vector.tensor_scalar_mul(out=r_30th[:], in0=r[:], scalar1=1.0 / 30.0)
        odd = small("odd")
        add_mult(odd, r2, 420.0, r2)
        even = small("even")
        add_mult(even, r2, 112.0, r2)
        add_mult(odd, odd, 15120.0, r_30th)
        e_num = small("e_num")
        nc.vector.scalar_tensor_tensor(
            out=e_num[:], in0=even[:], scalar=1008.0, in1=odd[:], op0=ALU.add, op1=ALU.add
        )
        e_den = small("e_den")
        nc.vector.scalar_tensor_tensor(
            out=e_den[:], in0=even[:], scalar=1008.0, in1=odd[:], op0=ALU.add, op1=ALU.subtract
        )
        nc.vector.tensor_mul(out=e_num[:], in0=e_num[:], in1=two_to_power[:].bitcast(F32))
        nc.vector.tensor_copy(out=edges_rows[0 : 2 * N, :], in_=edges_b[:])
        edges_t = bank_pool.tile([P, P], F32, tag="bank")
        nc.tensor.transpose(out=edges_t[:], in_=edges_rows[:], identity=ident_f[:])
        z = small("z")
        nc.vector.scalar_tensor_tensor(
            out=z[:], in0=e_den[:], scalar=2.0, in1=e_num[:], op0=ALU.mult, op1=ALU.add
        )
        nc.vector.reciprocal(out=z[:], in_=z[:])
        nc.vector.tensor_mul(out=z[:], in0=z[:], in1=e_num[:])
        y = small("y")
        nc.vector.tensor_mul(out=y[:], in0=z[:], in1=z[:])
        bottom = small("bottom")
        nc.vector.tensor_scalar_mul(out=bottom[:], in0=y[:], scalar1=225.0)
        top = small("top")
        nc.vector.tensor_scalar_mul(out=top[:], in0=y[:], scalar1=64.0)
        add_mult(bottom, bottom, -1050.0, y)
        add_mult(top, top, -735.0, y)
        nc.vector.tensor_scalar_add(out=bottom[:], in0=bottom[:], scalar1=945.0)
        add_mult(top, top, 945.0, z)
        right_bottom = small("right_bottom")
        nc.vector.tensor_mul(out=right_bottom[:], in0=edges_t[:, 0:N], in1=bottom[:])
        nc.vector.tensor_mul(out=kappa_relu[:], in0=kappa_relu[:], in1=bottom[:])
        inv_k = small("inv_k")
        nc.vector.scalar_tensor_tensor(
            out=inv_k[:], in0=top[:], scalar=2.0, in1=kappa_relu[:], op0=ALU.mult, op1=ALU.add
        )
        nc.vector.reciprocal(out=inv_k[:], in_=inv_k[:])
        neg_inv_k = small("neg_inv_k")
        nc.vector.scalar_tensor_tensor(
            out=neg_inv_k[:], in0=inv_k[:], scalar=-1.0, in1=bottom[:], op0=ALU.mult, op1=ALU.mult
        )
        bias_right = small("bias_right")
        nc.vector.tensor_mul(out=bias_right[:], in0=right_bottom[:], in1=inv_k[:])
        nc.vector.tensor_mul(out=inv_k[:], in0=inv_k[:], in1=bottom[:])
        bias_left = small("bias_left")
        nc.vector.tensor_mul(out=bias_left[:], in0=edges_t[:, N : 2 * N], in1=neg_inv_k[:])

        x_grouped = {}
        x_q = {}

        def regroup_x(piece):
            if piece not in x_grouped:
                grouped = xg_pool.tile([P, X_PASSES, B, F, PACK], BF16, align_bytes=64)
                x_grouped[piece] = grouped
            rows = slice(HEAD_ROWS if piece == 0 else 0, X_PASSES * B)
            copy_rows(nc.vector.tensor_copy, piece, rows)
            load_x(piece + X_LOADS)

        def copy_rows(copy, piece, rows):
            dst = x_grouped[piece][:].rearrange("p c b (r i) j -> p (c b) r j i", i=4)
            src = x_raw[piece][:].rearrange("p c b (j r i) -> p (c b) r j i", j=PACK, i=4)
            copy(out=dst[:, rows], in_=src[:, rows])

        head = xg_pool.tile([P, X_PASSES, B, F, PACK], BF16, align_bytes=64, name="grouped")
        x_grouped[0] = head
        copy_rows(nc.scalar.copy, 0, slice(0, HEAD_ROWS))

        def quantise(pool, grouped_flat, words):
            codes = pool.tile([P, UNIT_PASSES * P], U32, align_bytes=64)
            scales = pool.tile([P, UNIT_PASSES * P], U8, align_bytes=64)
            nc.vector.quantize_mx(
                out=codes[:, 0:words].bitcast(FP8X4), scales=scales[:, 0:words], in_=grouped_flat
            )
            return codes, scales

        def quantise_x(piece):
            flat = x_grouped[piece][:].rearrange("p c b f j -> p (c b f j)")
            x_q[piece] = quantise(xq_pool, flat, X_PASSES * P)

        steps = []
        units = []
        for n in range(N):
            widths = STEPS
            if n == 0:
                widths = FIRST_STEPS
            if n == N - 1:
                widths = LAST_STEPS
            first = 0
            for place in range(len(widths)):
                steps.append((n, place, first, widths[place]))
                unit = min(widths[place], UNIT_PASSES)
                units.append([(start, unit) for start in range(0, widths[place], unit)])
                first += widths[place]

        def units_of(step):
            return [(step, start, size) for start, size in units[step]] if 0 <= step < len(steps) else []

        sigmoids = {}

        def sigmoid(step, pool, bias, scale, name):
            n, place, first, width = steps[step]
            cols = width * PASS_TIMES
            tile = pool.tile([P, STEP_TIMES], F32, name=name)
            nc.scalar.activation(
                out=tile[:, 0:cols], in_=times[:, first * PASS_TIMES : first * PASS_TIMES + cols],
                func=FUNC.Sigmoid, bias=bias[:, n : n + 1], scale=scale[:, n : n + 1],
            )
            sigmoids[(step, name)] = tile

        alpha = {}
        partial = const.tile([P, N, MOST_STEPS], F32)
        nc.vector.memset(partial[:], 0.0)

        def product(step):
            n, place, first, width = steps[step]
            cols = width * PASS_TIMES
            rounded = alpha_pool.tile([P, STEP_TIMES], BF16, align_bytes=64)
            nc.vector.scalar_tensor_tensor(
                out=rounded[:, 0:cols], in0=sigmoids[(step, "fall")][:, 0:cols], scalar=1.0,
                in1=sigmoids[(step, "rise")][:, 0:cols], op0=ALU.mult, op1=ALU.mult,
                accum_out=partial[:, n, place : place + 1],
            )
            alpha[step] = rounded

        banks = {}

        def transpose(unit):
            step, start, size = unit
            words = alpha[step][:].bitcast(F32)
            for side in range(0, size, BANK_PASSES):
                bank = bank_pool.tile([P, BANK_PASSES, PAIR, M], F32, tag="bank")
                for c in range(min(size, BANK_PASSES)):
                    word = (start + side + c) * PASS_WORDS
                    for u in range(PAIR):
                        nc.tensor.transpose(
                            out=bank[:, c, u, :],
                            in_=words[:, word + u : word + PASS_WORDS : PAIR],
                            identity=ident_f[:],
                        )
                banks[(unit, side)] = bank

        alpha_grouped = {}
        alpha_q = {}

        def empty_banks(unit):
            step, start, size = unit
            grouped = ag_pool.tile([P, UNIT_PASSES * M * PACK], BF16, align_bytes=64)
            words = grouped[:].bitcast(F32).rearrange("p (c m u) -> p c m u", m=M, u=PAIR)
            for side in range(0, size, BANK_PASSES):
                end = side + min(size, BANK_PASSES)
                dst = words[:, side:end]
                src = banks[(unit, side)][:, 0 : end - side].rearrange("p c u m -> p c m u")
                if side < BANK_PASSES * SCALAR_BANKS[step % len(SCALAR_BANKS)]:
                    nc.scalar.copy(out=dst, in_=src)
                else:
                    nc.vector.tensor_copy(out=dst, in_=src)
            alpha_grouped[unit] = grouped

        def quantise_alpha(unit):
            step, start, size = unit
            flat = alpha_grouped[unit][:, 0 : size * M * PACK]
            alpha_q[unit] = quantise(aq_pool, flat, size * M)

        numerators = {}

        def set_of(n):
            return [channels for channels in SETS if channels[0] <= n < channels[1]][0]

        def multiply(unit):
            step, start, size = unit
            n, place, first, width = steps[step]
            begin, end = set_of(n)
            if n == begin and first + start == 0:
                numerator = sum_pool.tile([P, MOST_SET, B * F], F32, tag="numerator")
                numerators[begin] = numerator
            a_codes, a_scales = alpha_q[unit]
            for c in range(size):
                passed = first + start + c
                piece, part = divmod(n * PASSES_PER_N + passed, X_PASSES)
                x_codes, x_scales = x_q[piece]
                a_words = slice(c * P, (c + 1) * P)
                x_words = slice(part * P, (part + 1) * P)
                nc.tensor.matmul_mx(
                    out=numerators[begin][:, n - begin, :],
                    lhsT=a_codes[:, a_words].bitcast(FP8X4),
                    lhsT_scale=a_scales[:, a_words],
                    rhs=x_codes[:, x_words].bitcast(FP8X4),
                    rhs_scale=x_scales[:, x_words],
                    start=(passed == 0),
                    stop=(passed == PASSES_PER_N - 1),
                )

        inv_den = const.tile([P, N], F32)

        def invert_denominators(begin, end):
            nc.vector.tensor_reduce(
                out=inv_den[:, begin:end], in_=partial[:, begin:end], axis=AXIS_X, op=ALU.add
            )
            nc.vector.tensor_scalar_add(
                out=inv_den[:, begin:end], in0=inv_den[:, begin:end], scalar1=EPS
            )
            nc.vector.reciprocal(out=inv_den[:, begin:end], in_=inv_den[:, begin:end])

        def divide_and_store(begin, end):
            count = end - begin
            result = const.tile([P, count, B, F], F32, name="result%d" % begin)
            nc.vector.tensor_tensor(
                out=result[:].rearrange("m n b f -> m n (b f)"),
                in0=numerators[begin][:, 0:count],
                in1=inv_den[:, begin:end].unsqueeze(2).to_broadcast([P, count, B * F]),
                op=ALU.mult,
            )
            for b in range(B):
                nc.sync.dma_start(
                    out=out[b, begin:end].rearrange("n m f -> m n f"), in_=result[:, :, b, :]
                )

        x_regrouped = 0
        x_quantised = 0
        for turn in range(len(steps) + 2):
            if turn < len(steps):
                sigmoid(turn, fall_pool, bias_right, neg_inv_k, "fall")
            for unit in units_of(turn - 2):
                empty_banks(unit)
            if turn < len(steps):
                sigmoid(turn, rise_pool, bias_left, inv_k, "rise")
            for unit in units_of(turn - 1):
                transpose(unit)
            wanted = X_PIECES
            if turn == 0:
                wanted = 0
            elif turn < len(steps):
                n, place, first, width = steps[turn]
                passes = n * PASSES_PER_N + first + width
                wanted = (passes + X_PASSES - 1) // X_PASSES
            pending = units_of(turn - 2)
            while pending or x_quantised < wanted:
                if x_quantised < x_regrouped:
                    quantise_x(x_quantised)
                    x_quantised += 1
                if pending:
                    quantise_alpha(pending.pop(0))
                if x_regrouped < X_PIECES and x_regrouped < wanted + 1:
                    regroup_x(x_regrouped)
                    x_regrouped += 1
            for unit in units_of(turn - 2):
                multiply(unit)
            if turn < len(steps):
                product(turn)
                n, place, first, width = steps[turn]
                begin, end = set_of(n)
                if first + width == PASSES_PER_N and n + 1 == end:
                    invert_denominators(begin, end)
            if 2 <= turn:
                n, place, first, width = steps[turn - 2]
                begin, end = set_of(n)
                if first + width == PASSES_PER_N and n + 1 == end:
                    divide_and_store(begin, end)
